import numpy as np
import ml_dtypes


def mxq(x, axis, fmt="e4m3"):
    dtype, down = {"e4m3": (ml_dtypes.float8_e4m3fn, 7), "e5m2": (ml_dtypes.float8_e5m2, 14)}[fmt]
    v = np.moveaxis(np.asarray(x, np.float32).astype(ml_dtypes.bfloat16).astype(np.float64), axis, -1)
    blocks = v.reshape(v.shape[:-1] + (-1, 32))
    amax = np.abs(blocks).max(-1, keepdims=True)
    byte = np.maximum(np.where(amax > 0, np.frexp(amax)[1] - 1 + 127, 0) - down, 1)
    scale = np.exp2(byte - 127.0)
    codes = (blocks / scale).astype(np.float32).astype(dtype).astype(np.float64)
    return np.moveaxis((codes * scale).reshape(v.shape), -1, axis)


WIDE = False


def mx_kscale(k):
    if not WIDE:
        return np.ones(k)
    levels = np.array([10, -10, 5, -5, 0])
    a = np.random.permutation(np.resize(levels, k // 512 * 4)).reshape(k // 512, 4)
    idx = np.arange(k)
    return np.exp2(a[idx // 512, idx % 128 // 32])


BF16 = ml_dtypes.bfloat16


def bf(x):
    return np.asarray(x, np.float32).astype(BF16)


def f64(x):
    return np.asarray(x).astype(np.float64)


B, S, H, E, V, G, P = 4, 128, 1024, 512, 2048, 5, 3
C = G + P
EPS = 1e-12
KNOTS = np.linspace(-1.0 - 2.0 / G * P, 1.0 + 2.0 / G * P, G + 2 * P + 1)


def silu(v):
    e = np.exp(-np.abs(v))
    return v * np.where(v >= 0.0, 1.0, e) / (1.0 + e)


def erf(v):
    u = np.clip(v, -6.0, 6.0)
    term = u.copy()
    total = u.copy()
    for n in range(1, 200):
        term = term * (2.0 * u * u / (2.0 * n + 1.0))
        total = total + term
    return 2.0 / np.sqrt(np.pi) * np.exp(-u * u) * total


def gelu_erf(v):
    return 0.5 * v * (1.0 + erf(v / np.sqrt(2.0)))


def b_splines(x):
    xe = x[..., None]
    bases = np.where((xe >= KNOTS[:-1]) & (xe < KNOTS[1:]), 1.0, 0.0)
    for p in range(1, P + 1):
        left = (xe - KNOTS[: -(p + 1)]) / (KNOTS[p:-1] - KNOTS[: -(p + 1)])
        right = (KNOTS[p + 1:] - xe) / (KNOTS[p + 1:] - KNOTS[1:-p])
        bases = left * bases[..., :-1] + right * bases[..., 1:]
    return bases


def setup_inputs():
    s = mx_kscale(H)
    u = s / s.min()
    return {"hidden": bf(np.random.standard_normal((B, S, H)) * u),
            "base_w1": bf(np.random.standard_normal((E, H)) / np.sqrt(H) / u),
            "spline_w1": bf(np.random.standard_normal((E, H, C)) / np.sqrt(H))}


def reference(hidden, base_w1, spline_w1):
    x = f64(hidden).reshape(B * S, H)
    base = mxq(silu(x), 1, "e4m3") @ mxq(f64(base_w1), 1, "e4m3").T
    spl = mxq(b_splines(x).reshape(B * S, H * C), 1, "e4m3") @ mxq(f64(spline_w1).reshape(E, H * C), 1, "e4m3").T
    g = gelu_erf(base + spl)
    mu = g.mean(-1, keepdims=True)
    var = np.square(g - mu).mean(-1, keepdims=True)
    return ((g - mu) / np.sqrt(var + EPS)).reshape(B, S, E)

@@ -1,0 +1,192 @@
+from contextlib import ExitStack
+
+import concourse.mybir as mybir
+from concourse.masks import make_identity
+
+F32 = mybir.dt.float32
+BF16 = mybir.dt.bfloat16
+U32 = mybir.dt.uint32
+U8 = mybir.dt.uint8
+FP8X4 = mybir.dt.float8_e4m3fn_x4
+ACT = mybir.ActivationFunctionType
+ALU = mybir.AluOpType
+
+P = 128
+PACK = 4
+TOKENS = 512
+FEATURES = 1024
+OUTS = 512
+BASIS = 8
+TOKEN_TILES = TOKENS // P
+OUT_TILES = OUTS // P
+FEATURE_TILES = FEATURES // P
+BASE_PASSES = FEATURES // (P * PACK)
+HALF_OUTS = OUTS // 2
+EPS = 1e-12
+KNOT_STEP = 0.4
+FIRST_KNOT = -2.2
+
+FLOPS = 2 * TOKENS * OUTS * (FEATURES + FEATURES * BASIS)
+
+
+def quantise(nc, pool, grouped_bf16, width, label):
+    codes = pool.tile([P, width], U32, align_bytes=64, name=label + "_codes")
+    scales = pool.tile([P, width], U8, align_bytes=64, name=label + "_scales")
+    nc.vector.quantize_mx(out=codes[:].bitcast(FP8X4), scales=scales[:], in_=grouped_bf16)
+    return codes, scales
+
+
+def multiply(nc, acc, acts, weights, start, stop):
+    act_codes, act_scales = acts
+    w_codes, w_scales = weights
+    for m in range(TOKEN_TILES):
+        cols = slice(m * P, (m + 1) * P)
+        nc.tensor.matmul_mx(
+            out=acc[m][:],
+            lhsT=act_codes[:, cols].bitcast(FP8X4),
+            lhsT_scale=act_scales[:, cols],
+            rhs=w_codes[:].bitcast(FP8X4),
+            rhs_scale=w_scales[:],
+            start=start,
+            stop=stop,
+        )
+
+
+def tile_generatorhead_pa_kernel(tc, hidden, base_w1, spline_w1, out):
+    nc = tc.nc
+    x_rows = hidden.flatten_outer_dims().rearrange("(m p) i -> p m i", p=P)
+    base_rows = base_w1.rearrange("(n p) i -> p n i", p=P)
+    spline_rows = spline_w1.rearrange("(n p) i c -> p n (i c)", p=P)
+    out_rows = out.flatten_outer_dims()
+
+    with ExitStack() as ctx:
+        keep = ctx.enter_context(tc.tile_pool(name="keep", bufs=1))
+        wload = ctx.enter_context(tc.tile_pool(name="wload", bufs=3))
+        work = ctx.enter_context(tc.tile_pool(name="work", bufs=2))
+        mx = ctx.enter_context(tc.tile_pool(name="mx", bufs=2))
+        acc_pool = ctx.enter_context(tc.psum_pool(name="acc", bufs=1))
+        turn = ctx.enter_context(tc.psum_pool(name="turn", bufs=4))
+
+        ident_bf = keep.tile([P, P], BF16)
+        make_identity(nc, ident_bf[:])
+        ident_f32 = keep.tile([P, P], F32)
+        make_identity(nc, ident_f32[:])
+
+        x_tok = keep.tile([P, TOKEN_TILES, FEATURES], BF16)
+        for m in range(TOKEN_TILES):
+            nc.sync.dma_start(out=x_tok[:, m, :], in_=x_rows[:, m, :])
+        base_raw = keep.tile([P, OUT_TILES, FEATURES], BF16)
+        nc.sync.dma_start(out=base_raw[:], in_=base_rows)
+
+        acc = [acc_pool.tile([P, OUTS], F32, name="acc%d" % m) for m in range(TOKEN_TILES)]
+
+        x_feat = keep.tile([P, FEATURE_TILES, TOKENS], BF16)
+        for pair in range(FEATURE_TILES // 2):
+            x_bank = turn.tile([P, 2, TOKENS], BF16, tag="bank")
+            for j in range(2):
+                a = 2 * pair + j
+                for m in range(TOKEN_TILES):
+                    nc.tensor.transpose(
+                        x_bank[:, j, m * P : (m + 1) * P], x_tok[:, m, a * P : (a + 1) * P], ident_bf[:]
+                    )
+            nc.vector.tensor_copy(out=x_feat[:, 2 * pair : 2 * pair + 2, :], in_=x_bank[:])
+
+        for g in range(BASE_PASSES):
+            silu_grouped = work.tile([P, TOKENS, PACK], BF16, align_bytes=64)
+            nc.scalar.activation(
+                out=silu_grouped[:],
+                in_=x_feat[:, PACK * g : PACK * (g + 1), :].rearrange("p t k -> p k t"),
+                func=ACT.Silu,
+            )
+            base_grouped = work.tile([P, OUTS, PACK], BF16, align_bytes=64)
+            for half in range(2):
+                base_bank = turn.tile([P, PACK, HALF_OUTS], BF16, tag="bank")
+                for t in range(PACK):
+                    a = PACK * g + t
+                    for j in range(2):
+                        nc.tensor.transpose(
+                            base_bank[:, t, j * P : (j + 1) * P],
+                            base_raw[:, 2 * half + j, a * P : (a + 1) * P],
+                            ident_bf[:],
+                        )
+                nc.vector.tensor_copy(
+                    out=base_grouped[:, half * HALF_OUTS : (half + 1) * HALF_OUTS, :],
+                    in_=base_bank[:].rearrange("p t o -> p o t"),
+                )
+            acts = quantise(nc, mx, silu_grouped[:].rearrange("p k t -> p (k t)"), TOKENS, "silu")
+            weights = quantise(nc, mx, base_grouped[:].rearrange("p o t -> p (o t)"), OUTS, "base")
+            multiply(nc, acc, acts, weights, start=(g == 0), stop=False)
+
+        for a in range(FEATURE_TILES):
+            w_raw = wload.tile([P, OUT_TILES, P * BASIS], BF16)
+            nc.sync.dma_start(out=w_raw[:], in_=spline_rows[:, :, a * P * BASIS : (a + 1) * P * BASIS])
+            w_words = w_raw[:].bitcast(F32).rearrange("p n (f w) -> p n f w", w=BASIS // 2)
+
+            x_a = x_feat[:, a, :]
+            dist = work.tile([P, PACK, TOKENS], F32)
+            for r in range(PACK):
+                nc.scalar.activation(out=dist[:, r, :], in_=x_a, func=ACT.Abs, scale=1.0 / KNOT_STEP, bias=1.5 - r)
+            nc.scalar.activation(out=dist[:], in_=dist[:], func=ACT.Abs, bias=-2.0)
+            neg_w = work.tile([P, PACK, TOKENS], F32)
+            nc.vector.tensor_scalar(out=neg_w[:], in0=dist[:], scalar1=2.0, scalar2=2.0, op0=ALU.min, op1=ALU.subtract)
+            inner = work.tile([P, PACK, TOKENS], F32)
+            nc.scalar.activation(out=inner[:], in_=neg_w[:], func=ACT.Square, bias=2.0)
+            outer = work.tile([P, PACK, TOKENS], F32)
+            nc.scalar.activation(out=outer[:], in_=neg_w[:], func=ACT.Square)
+            nc.vector.tensor_tensor(out=inner[:], in0=inner[:], in1=neg_w[:], op=ALU.mult)
+            nc.vector.scalar_tensor_tensor(
+                out=outer[:], in0=neg_w[:], scalar=-1.0 / 3.0, in1=outer[:], op0=ALU.mult, op1=ALU.mult
+            )
+            twice = work.tile([P, PACK, TOKENS], BF16)
+            nc.vector.scalar_tensor_tensor(
+                out=twice[:], in0=inner[:], scalar=4.0 / 3.0, in1=outer[:], op0=ALU.add, op1=ALU.min
+            )
+            side = work.tile([P, PACK, TOKENS], BF16)
+            for r in range(PACK):
+                nc.vector.tensor_scalar(
+                    out=side[:, r, :],
+                    in0=x_a,
+                    scalar1=FIRST_KNOT + KNOT_STEP * (r + PACK),
+                    scalar2=0.5,
+                    op0=ALU.is_ge,
+                    op1=ALU.subtract,
+                )
+            nc.vector.tensor_tensor(out=twice[:], in0=twice[:], in1=side[:], op=ALU.mult)
+            signed = twice[:].rearrange("p r k -> p k r")
+            low = work.tile([P, TOKENS, PACK], BF16, align_bytes=64)
+            nc.vector.tensor_scalar(out=low[:], in0=signed, scalar1=-1.0, scalar2=0.0, op0=ALU.mult, op1=ALU.max)
+            high = work.tile([P, TOKENS, PACK], BF16, align_bytes=64)
+            nc.vector.tensor_scalar(out=high[:], in0=signed, scalar1=0.0, scalar2=None, op0=ALU.max)
+
+            for h, basis_grouped in enumerate((low, high)):
+                w_grouped = work.tile([P, OUTS, 2], F32, align_bytes=64)
+                for half in range(2):
+                    w_bank = turn.tile([P, 2, HALF_OUTS], F32, tag="bank")
+                    for u in range(2):
+                        for j in range(2):
+                            nc.tensor.transpose(
+                                w_bank[:, u, j * P : (j + 1) * P], w_words[:, 2 * half + j, :, 2 * h + u], ident_f32[:]
+                            )
+                    nc.scalar.copy(
+                        out=w_grouped[:, half * HALF_OUTS : (half + 1) * HALF_OUTS, :],
+                        in_=w_bank[:].rearrange("p u o -> p o u"),
+                    )
+                acts = quantise(nc, mx, basis_grouped[:].rearrange("p k t -> p (k t)"), TOKENS, "basis")
+                weights = quantise(nc, mx, w_grouped[:].rearrange("p o u -> p (o u)").bitcast(BF16), OUTS, "spline")
+                multiply(nc, acc, acts, weights, start=False, stop=(a == FEATURE_TILES - 1 and h == 1))
+
+        for m in range(TOKEN_TILES):
+            gelu = work.tile([P, OUTS], F32)
+            nc.scalar.activation(out=gelu[:], in_=acc[m][:], func=ACT.Gelu)
+            stats = work.tile([P, 6], F32)
+            nc.vector.bn_stats(out=stats[:], in_=gelu[:])
+            mean_var = work.tile([P, 2], F32)
+            nc.vector.bn_aggr(out=mean_var[:], in_=stats[:])
+            rstd = work.tile([P, 1], F32)
+            nc.scalar.activation(out=rstd[:], in_=mean_var[:, 1:2], func=ACT.Sqrt, bias=EPS)
+            nc.vector.reciprocal(out=rstd[:], in_=rstd[:])
+            normed = work.tile([P, OUTS], F32)
+            nc.vector.tensor_scalar(
+                out=normed[:], in0=gelu[:], scalar1=mean_var[:, 0:1], scalar2=rstd[:], op0=ALU.subtract, op1=ALU.mult
+            )
+            nc.sync.dma_start(out=out_rows[m * P : (m + 1) * P, :], in_=normed[:])

@@ -19,7 +19,7 @@ OUTS = 512
 BASIS = 8
 TOKEN_TILES = TOKENS // P
 OUT_TILES = OUTS // P
-FEATURE_TILES = FEATURES // P
+CHUNKS = FEATURES // P
 BASE_PASSES = FEATURES // (P * PACK)
 HALF_OUTS = OUTS // 2
 EPS = 1e-12
@@ -27,29 +27,6 @@ KNOT_STEP = 0.4
 FIRST_KNOT = -2.2
 
 FLOPS = 2 * TOKENS * OUTS * (FEATURES + FEATURES * BASIS)
-
-
-def quantise(nc, pool, grouped_bf16, width, label):
-    codes = pool.tile([P, width], U32, align_bytes=64, name=label + "_codes")
-    scales = pool.tile([P, width], U8, align_bytes=64, name=label + "_scales")
-    nc.vector.quantize_mx(out=codes[:].bitcast(FP8X4), scales=scales[:], in_=grouped_bf16)
-    return codes, scales
-
-
-def multiply(nc, acc, acts, weights, start, stop):
-    act_codes, act_scales = acts
-    w_codes, w_scales = weights
-    for m in range(TOKEN_TILES):
-        cols = slice(m * P, (m + 1) * P)
-        nc.tensor.matmul_mx(
-            out=acc[m][:],
-            lhsT=act_codes[:, cols].bitcast(FP8X4),
-            lhsT_scale=act_scales[:, cols],
-            rhs=w_codes[:].bitcast(FP8X4),
-            rhs_scale=w_scales[:],
-            start=start,
-            stop=stop,
-        )
 
 
 def tile_generatorhead_pa_kernel(tc, hidden, base_w1, spline_w1, out):
@@ -66,22 +43,127 @@ def tile_generatorhead_pa_kernel(tc, hidden, base_w1, spline_w1, out):
         mx = ctx.enter_context(tc.tile_pool(name="mx", bufs=2))
         acc_pool = ctx.enter_context(tc.psum_pool(name="acc", bufs=1))
         turn = ctx.enter_context(tc.psum_pool(name="turn", bufs=4))
-
-        ident_bf = keep.tile([P, P], BF16)
-        make_identity(nc, ident_bf[:])
-        ident_f32 = keep.tile([P, P], F32)
-        make_identity(nc, ident_f32[:])
+        ctx.enter_context(tc.manual_schedule())
 
         x_tok = keep.tile([P, TOKEN_TILES, FEATURES], BF16)
-        for m in range(TOKEN_TILES):
-            nc.sync.dma_start(out=x_tok[:, m, :], in_=x_rows[:, m, :])
+        x_feat = keep.tile([P, CHUNKS, TOKENS], BF16)
         base_raw = keep.tile([P, OUT_TILES, FEATURES], BF16)
-        nc.sync.dma_start(out=base_raw[:], in_=base_rows)
-
         acc = [acc_pool.tile([P, OUTS], F32, name="acc%d" % m) for m in range(TOKEN_TILES)]
+        w_raw = {}
+        dist = {}
+        neg_w = {}
+        inner = {}
+        outer = {}
+        side = {}
+        signed = {}
+        grouped = {}
+        quantised = {}
 
-        x_feat = keep.tile([P, FEATURE_TILES, TOKENS], BF16)
-        for pair in range(FEATURE_TILES // 2):
+        def load_weights(a):
+            w_raw[a] = wload.tile([P, OUT_TILES, P * BASIS], BF16, name="w_raw")
+            nc.sync.dma_start(out=w_raw[a][:], in_=spline_rows[:, :, a * P * BASIS : (a + 1) * P * BASIS])
+
+        def quantise(key, grouped_bf16, width):
+            codes = mx.tile([P, width], U32, align_bytes=64, name=key[0] + "_codes")
+            scales = mx.tile([P, width], U8, align_bytes=64, name=key[0] + "_scales")
+            nc.vector.quantize_mx(out=codes[:].bitcast(FP8X4), scales=scales[:], in_=grouped_bf16)
+            quantised[key] = (codes, scales)
+
+        def multiply(act_key, w_key, start, stop):
+            act_codes, act_scales = quantised[act_key]
+            w_codes, w_scales = quantised[w_key]
+            for m in range(TOKEN_TILES):
+                cols = slice(m * P, (m + 1) * P)
+                nc.tensor.matmul_mx(
+                    out=acc[m][:],
+                    lhsT=act_codes[:, cols].bitcast(FP8X4),
+                    lhsT_scale=act_scales[:, cols],
+                    rhs=w_codes[:].bitcast(FP8X4),
+                    rhs_scale=w_scales[:],
+                    start=start,
+                    stop=stop,
+                )
+
+        def distances(a):
+            dist[a] = work.tile([P, PACK, TOKENS], F32, name="dist")
+            for r in range(PACK):
+                nc.scalar.activation(
+                    out=dist[a][:, r, :], in_=x_feat[:, a, :], func=ACT.Abs, scale=1.0 / KNOT_STEP, bias=1.5 - r
+                )
+            nc.scalar.activation(out=dist[a][:], in_=dist[a][:], func=ACT.Abs, bias=-2.0)
+
+        def clamp(a):
+            neg_w[a] = work.tile([P, PACK, TOKENS], F32, name="neg_w")
+            nc.vector.tensor_scalar(
+                out=neg_w[a][:], in0=dist[a][:], scalar1=2.0, scalar2=2.0, op0=ALU.min, op1=ALU.subtract
+            )
+
+        def sides(a):
+            side[a] = work.tile([P, PACK, TOKENS], BF16, name="side")
+            for r in range(PACK):
+                nc.vector.tensor_scalar(
+                    out=side[a][:, r, :],
+                    in0=x_feat[:, a, :],
+                    scalar1=FIRST_KNOT + KNOT_STEP * (r + PACK),
+                    scalar2=0.5,
+                    op0=ALU.is_ge,
+                    op1=ALU.subtract,
+                )
+
+        def squares(a):
+            inner[a] = work.tile([P, PACK, TOKENS], F32, name="inner")
+            nc.scalar.activation(out=inner[a][:], in_=neg_w[a][:], func=ACT.Square, bias=2.0)
+            outer[a] = work.tile([P, PACK, TOKENS], F32, name="outer")
+            nc.scalar.activation(out=outer[a][:], in_=neg_w[a][:], func=ACT.Square)
+
+        def cubics(a):
+            nc.vector.tensor_tensor(out=inner[a][:], in0=inner[a][:], in1=neg_w[a][:], op=ALU.mult)
+            nc.vector.scalar_tensor_tensor(
+                out=outer[a][:], in0=neg_w[a][:], scalar=-1.0 / 3.0, in1=outer[a][:], op0=ALU.mult, op1=ALU.mult
+            )
+            signed[a] = work.tile([P, PACK, TOKENS], BF16, name="signed")
+            nc.vector.scalar_tensor_tensor(
+                out=signed[a][:], in0=inner[a][:], scalar=4.0 / 3.0, in1=outer[a][:], op0=ALU.add, op1=ALU.min
+            )
+            nc.vector.tensor_tensor(out=signed[a][:], in0=signed[a][:], in1=side[a][:], op=ALU.mult)
+
+        def high_half(a):
+            grouped[a, 1] = work.tile([P, TOKENS, PACK], BF16, align_bytes=64, name="high")
+            nc.scalar.activation(out=grouped[a, 1][:], in_=signed[a][:].rearrange("p r k -> p k r"), func=ACT.Relu)
+
+        def low_half(a):
+            grouped[a, 0] = work.tile([P, TOKENS, PACK], BF16, align_bytes=64, name="low")
+            nc.vector.tensor_scalar(
+                out=grouped[a, 0][:],
+                in0=signed[a][:].rearrange("p r k -> p k r"),
+                scalar1=-1.0,
+                scalar2=0.0,
+                op0=ALU.mult,
+                op1=ALU.max,
+            )
+
+        def turn_weights(a):
+            w_words = w_raw[a][:].bitcast(F32).rearrange("p n (f w) -> p n f w", w=BASIS // 2)
+            banks = {}
+            for h in range(2):
+                for half in range(2):
+                    banks[h, half] = turn.tile([P, 2, HALF_OUTS], F32, tag="bank", name="w_bank")
+                    for u in range(2):
+                        for j in range(2):
+                            nc.tensor.transpose(
+                                banks[h, half][:, u, j * P : (j + 1) * P],
+                                w_words[:, 2 * half + j, :, 2 * h + u],
+                                ident_f32[:],
+                            )
+            for h in range(2):
+                grouped["w", a, h] = work.tile([P, OUTS, 2], F32, align_bytes=64, name="w_grouped%d" % h)
+                for half in range(2):
+                    nc.scalar.copy(
+                        out=grouped["w", a, h][:, half * HALF_OUTS : (half + 1) * HALF_OUTS, :],
+                        in_=banks[h, half][:].rearrange("p u o -> p o u"),
+                    )
+
+        def turn_x(pair):
             x_bank = turn.tile([P, 2, TOKENS], BF16, tag="bank")
             for j in range(2):
                 a = 2 * pair + j
@@ -91,14 +173,33 @@ def tile_generatorhead_pa_kernel(tc, hidden, base_w1, spline_w1, out):
                     )
             nc.vector.tensor_copy(out=x_feat[:, 2 * pair : 2 * pair + 2, :], in_=x_bank[:])
 
+        def load_x(pair):
+            cols = slice(2 * pair * P, 2 * (pair + 1) * P)
+            nc.sync.dma_start(out=x_tok[:, :, cols], in_=x_rows[:, :, cols])
+
+        load_x(0)
+        load_x(1)
+        nc.sync.dma_start(out=base_raw[:], in_=base_rows)
+        load_x(2)
+        load_x(3)
+        for a in range(3):
+            load_weights(a)
+
+        ident_bf = keep.tile([P, P], BF16)
+        make_identity(nc, ident_bf[:])
+        ident_f32 = keep.tile([P, P], F32)
+        make_identity(nc, ident_f32[:])
+
+        zero = keep.tile([P, 1], F32)
+        nc.vector.memset(zero[:], 0.0)
+        warm = keep.tile([P, 1], F32)
+        nc.scalar.activation(out=warm[:], in_=zero[:], func=ACT.Silu)
+
+
         for g in range(BASE_PASSES):
-            silu_grouped = work.tile([P, TOKENS, PACK], BF16, align_bytes=64)
-            nc.scalar.activation(
-                out=silu_grouped[:],
-                in_=x_feat[:, PACK * g : PACK * (g + 1), :].rearrange("p t k -> p k t"),
-                func=ACT.Silu,
-            )
-            base_grouped = work.tile([P, OUTS, PACK], BF16, align_bytes=64)
+            turn_x(2 * g)
+            turn_x(2 * g + 1)
+            grouped["base", g] = work.tile([P, OUTS, PACK], BF16, align_bytes=64, name="base_grouped")
             for half in range(2):
                 base_bank = turn.tile([P, PACK, HALF_OUTS], BF16, tag="bank")
                 for t in range(PACK):
@@ -110,83 +211,67 @@ def tile_generatorhead_pa_kernel(tc, hidden, base_w1, spline_w1, out):
                             ident_bf[:],
                         )
                 nc.vector.tensor_copy(
-                    out=base_grouped[:, half * HALF_OUTS : (half + 1) * HALF_OUTS, :],
+                    out=grouped["base", g][:, half * HALF_OUTS : (half + 1) * HALF_OUTS, :],
                     in_=base_bank[:].rearrange("p t o -> p o t"),
                 )
-            acts = quantise(nc, mx, silu_grouped[:].rearrange("p k t -> p (k t)"), TOKENS, "silu")
-            weights = quantise(nc, mx, base_grouped[:].rearrange("p o t -> p (o t)"), OUTS, "base")
-            multiply(nc, acc, acts, weights, start=(g == 0), stop=False)
-
-        for a in range(FEATURE_TILES):
-            w_raw = wload.tile([P, OUT_TILES, P * BASIS], BF16)
-            nc.sync.dma_start(out=w_raw[:], in_=spline_rows[:, :, a * P * BASIS : (a + 1) * P * BASIS])
-            w_words = w_raw[:].bitcast(F32).rearrange("p n (f w) -> p n f w", w=BASIS // 2)
-
-            x_a = x_feat[:, a, :]
-            dist = work.tile([P, PACK, TOKENS], F32)
-            for r in range(PACK):
-                nc.scalar.activation(out=dist[:, r, :], in_=x_a, func=ACT.Abs, scale=1.0 / KNOT_STEP, bias=1.5 - r)
-            nc.scalar.activation(out=dist[:], in_=dist[:], func=ACT.Abs, bias=-2.0)
-            neg_w = work.tile([P, PACK, TOKENS], F32)
-            nc.vector.tensor_scalar(out=neg_w[:], in0=dist[:], scalar1=2.0, scalar2=2.0, op0=ALU.min, op1=ALU.subtract)
-            inner = work.tile([P, PACK, TOKENS], F32)
-            nc.scalar.activation(out=inner[:], in_=neg_w[:], func=ACT.Square, bias=2.0)
-            outer = work.tile([P, PACK, TOKENS], F32)
-            nc.scalar.activation(out=outer[:], in_=neg_w[:], func=ACT.Square)
-            nc.vector.tensor_tensor(out=inner[:], in0=inner[:], in1=neg_w[:], op=ALU.mult)
-            nc.vector.scalar_tensor_tensor(
-                out=outer[:], in0=neg_w[:], scalar=-1.0 / 3.0, in1=outer[:], op0=ALU.mult, op1=ALU.mult
+        distances(0)
+        clamp(0)
+        sides(0)
+        for g in range(BASE_PASSES):
+            quantise(("base", g), grouped["base", g][:].rearrange("p o t -> p (o t)"), OUTS)
+        for g in range(BASE_PASSES):
+            grouped["silu", g] = work.tile([P, TOKENS, PACK], BF16, align_bytes=64, name="silu_grouped")
+            nc.scalar.activation(
+                out=grouped["silu", g][:],
+                in_=x_feat[:, PACK * g : PACK * (g + 1), :].rearrange("p t k -> p k t"),
+                func=ACT.Silu,
             )
-            twice = work.tile([P, PACK, TOKENS], BF16)
-            nc.vector.scalar_tensor_tensor(
-                out=twice[:], in0=inner[:], scalar=4.0 / 3.0, in1=outer[:], op0=ALU.add, op1=ALU.min
-            )
-            side = work.tile([P, PACK, TOKENS], BF16)
-            for r in range(PACK):
-                nc.vector.tensor_scalar(
-                    out=side[:, r, :],
-                    in0=x_a,
-                    scalar1=FIRST_KNOT + KNOT_STEP * (r + PACK),
-                    scalar2=0.5,
-                    op0=ALU.is_ge,
-                    op1=ALU.subtract,
-                )
-            nc.vector.tensor_tensor(out=twice[:], in0=twice[:], in1=side[:], op=ALU.mult)
-            signed = twice[:].rearrange("p r k -> p k r")
-            low = work.tile([P, TOKENS, PACK], BF16, align_bytes=64)
-            nc.vector.tensor_scalar(out=low[:], in0=signed, scalar1=-1.0, scalar2=0.0, op0=ALU.mult, op1=ALU.max)
-            high = work.tile([P, TOKENS, PACK], BF16, align_bytes=64)
-            nc.vector.tensor_scalar(out=high[:], in0=signed, scalar1=0.0, scalar2=None, op0=ALU.max)
+        squares(0)
+        distances(1)
+        turn_weights(0)
+        for g in range(BASE_PASSES):
+            quantise(("silu", g), grouped["silu", g][:].rearrange("p k t -> p (k t)"), TOKENS)
+            multiply(("silu", g), ("base", g), start=(g == 0), stop=False)
 
-            for h, basis_grouped in enumerate((low, high)):
-                w_grouped = work.tile([P, OUTS, 2], F32, align_bytes=64)
-                for half in range(2):
-                    w_bank = turn.tile([P, 2, HALF_OUTS], F32, tag="bank")
-                    for u in range(2):
-                        for j in range(2):
-                            nc.tensor.transpose(
-                                w_bank[:, u, j * P : (j + 1) * P], w_words[:, 2 * half + j, :, 2 * h + u], ident_f32[:]
-                            )
-                    nc.scalar.copy(
-                        out=w_grouped[:, half * HALF_OUTS : (half + 1) * HALF_OUTS, :],
-                        in_=w_bank[:].rearrange("p u o -> p o u"),
-                    )
-                acts = quantise(nc, mx, basis_grouped[:].rearrange("p k t -> p (k t)"), TOKENS, "basis")
-                weights = quantise(nc, mx, w_grouped[:].rearrange("p o u -> p (o u)").bitcast(BF16), OUTS, "spline")
-                multiply(nc, acc, acts, weights, start=False, stop=(a == FEATURE_TILES - 1 and h == 1))
+        for a in range(CHUNKS):
+            cubics(a)
+            high_half(a)
+            if a + 1 < CHUNKS:
+                clamp(a + 1)
+                squares(a + 1)
+            low_half(a)
+            if a + 1 < CHUNKS:
+                sides(a + 1)
+            if a + 2 < CHUNKS:
+                distances(a + 2)
+            if a + 3 < CHUNKS:
+                load_weights(a + 3)
+            if a + 1 < CHUNKS:
+                turn_weights(a + 1)
+            for h in range(2):
+                quantise(("basis", a, h), grouped[a, h][:].rearrange("p k t -> p (k t)"), TOKENS)
+                quantise(("spline", a, h), grouped["w", a, h][:].rearrange("p o u -> p (o u)").bitcast(BF16), OUTS)
+                multiply(("basis", a, h), ("spline", a, h), start=False, stop=(a == CHUNKS - 1 and h == 1))
 
+        nc.scalar.activation(out=warm[:], in_=zero[:], func=ACT.Gelu)
+        stats = keep.tile([P, TOKEN_TILES, 6], F32)
+        mean_var = keep.tile([P, TOKEN_TILES, 2], F32)
+        rstd = keep.tile([P, TOKEN_TILES], F32)
+        gelu = [keep.tile([P, OUTS], F32, name="gelu%d" % m) for m in range(TOKEN_TILES)]
         for m in range(TOKEN_TILES):
-            gelu = work.tile([P, OUTS], F32)
-            nc.scalar.activation(out=gelu[:], in_=acc[m][:], func=ACT.Gelu)
-            stats = work.tile([P, 6], F32)
-            nc.vector.bn_stats(out=stats[:], in_=gelu[:])
-            mean_var = work.tile([P, 2], F32)
-            nc.vector.bn_aggr(out=mean_var[:], in_=stats[:])
-            rstd = work.tile([P, 1], F32)
-            nc.scalar.activation(out=rstd[:], in_=mean_var[:, 1:2], func=ACT.Sqrt, bias=EPS)
-            nc.vector.reciprocal(out=rstd[:], in_=rstd[:])
-            normed = work.tile([P, OUTS], F32)
+            nc.scalar.activation(out=gelu[m][:], in_=acc[m][:], func=ACT.Gelu)
+            nc.vector.bn_stats(out=stats[:, m, :], in_=gelu[m][:])
+            nc.vector.bn_aggr(out=mean_var[:, m, :], in_=stats[:, m, :])
+        nc.scalar.activation(out=warm[:], in_=zero[:], func=ACT.Sqrt)
+        nc.scalar.activation(out=rstd[:], in_=mean_var[:, :, 1], func=ACT.Sqrt, bias=EPS)
+        nc.vector.reciprocal(out=rstd[:], in_=rstd[:])
+        for m in range(TOKEN_TILES):
             nc.vector.tensor_scalar(
-                out=normed[:], in0=gelu[:], scalar1=mean_var[:, 0:1], scalar2=rstd[:], op0=ALU.subtract, op1=ALU.mult
+                out=gelu[m][:],
+                in0=gelu[m][:],
+                scalar1=mean_var[:, m, 0:1],
+                scalar2=rstd[:, m : m + 1],
+                op0=ALU.subtract,
+                op1=ALU.mult,
             )
-            nc.sync.dma_start(out=out_rows[m * P : (m + 1) * P, :], in_=normed[:])
+            nc.sync.dma_start(out=out_rows[m * P : (m + 1) * P, :], in_=gelu[m][:])

@@ -26,6 +26,8 @@ EPS = 1e-12
 KNOT_STEP = 0.4
 FIRST_KNOT = -2.2
 
+RUN = 4
+
 FLOPS = 2 * TOKENS * OUTS * (FEATURES + FEATURES * BASIS)
 
 
@@ -129,13 +131,17 @@ def tile_generatorhead_pa_kernel(tc, hidden, base_w1, spline_w1, out):
 
         def high_half(a):
             grouped[a, 1] = work.tile([P, TOKENS, PACK], BF16, align_bytes=64, name="high")
-            nc.scalar.activation(out=grouped[a, 1][:], in_=signed[a][:].rearrange("p r k -> p k r"), func=ACT.Relu)
+            nc.scalar.activation(
+                out=grouped[a, 1][:].rearrange("p (c i) r -> p c r i", i=RUN),
+                in_=signed[a][:].rearrange("p r (c i) -> p c r i", i=RUN),
+                func=ACT.Relu,
+            )
 
         def low_half(a):
             grouped[a, 0] = work.tile([P, TOKENS, PACK], BF16, align_bytes=64, name="low")
             nc.vector.tensor_scalar(
-                out=grouped[a, 0][:],
-                in0=signed[a][:].rearrange("p r k -> p k r"),
+                out=grouped[a, 0][:].rearrange("p (c i) r -> p c r i", i=RUN),
+                in0=signed[a][:].rearrange("p r (c i) -> p c r i", i=RUN),
                 scalar1=-1.0,
                 scalar2=0.0,
                 op0=ALU.mult,
@@ -222,8 +228,8 @@ def tile_generatorhead_pa_kernel(tc, hidden, base_w1, spline_w1, out):
         for g in range(BASE_PASSES):
             grouped["silu", g] = work.tile([P, TOKENS, PACK], BF16, align_bytes=64, name="silu_grouped")
             nc.scalar.activation(
-                out=grouped["silu", g][:],
-                in_=x_feat[:, PACK * g : PACK * (g + 1), :].rearrange("p t k -> p k t"),
+                out=grouped["silu", g][:].rearrange("p (c i) t -> p c t i", i=RUN),
+                in_=x_feat[:, PACK * g : PACK * (g + 1), :].rearrange("p t (c i) -> p c t i", i=RUN),
                 func=ACT.Silu,
             )
         squares(0)

@@ -45,7 +45,6 @@ def tile_generatorhead_pa_kernel(tc, hidden, base_w1, spline_w1, out):
         mx = ctx.enter_context(tc.tile_pool(name="mx", bufs=2))
         acc_pool = ctx.enter_context(tc.psum_pool(name="acc", bufs=1))
         turn = ctx.enter_context(tc.psum_pool(name="turn", bufs=4))
-        ctx.enter_context(tc.manual_schedule())
 
         x_tok = keep.tile([P, TOKEN_TILES, FEATURES], BF16)
         x_feat = keep.tile([P, CHUNKS, TOKENS], BF16)
@@ -259,7 +258,7 @@ def tile_generatorhead_pa_kernel(tc, hidden, base_w1, spline_w1, out):
                 quantise(("spline", a, h), grouped["w", a, h][:].rearrange("p o u -> p (o u)").bitcast(BF16), OUTS)
                 multiply(("basis", a, h), ("spline", a, h), start=False, stop=(a == CHUNKS - 1 and h == 1))
 
-        nc.scalar.activation(out=warm[:], in_=zero[:], func=ACT.Gelu)
+        nc.scalar.activation(out=warm[:], in_=grouped[CHUNKS - 1, 1][:, 0, 0:1], func=ACT.Gelu)
         stats = keep.tile([P, TOKEN_TILES, 6], F32)
         mean_var = keep.tile([P, TOKEN_TILES, 2], F32)
         rstd = keep.tile([P, TOKEN_TILES], F32)
@@ -268,7 +267,7 @@ def tile_generatorhead_pa_kernel(tc, hidden, base_w1, spline_w1, out):
             nc.scalar.activation(out=gelu[m][:], in_=acc[m][:], func=ACT.Gelu)
             nc.vector.bn_stats(out=stats[:, m, :], in_=gelu[m][:])
             nc.vector.bn_aggr(out=mean_var[:, m, :], in_=stats[:, m, :])
-        nc.scalar.activation(out=warm[:], in_=zero[:], func=ACT.Sqrt)
+        nc.scalar.activation(out=warm[:], in_=gelu[TOKEN_TILES - 1][:, 0:1], func=ACT.Sqrt, scale=0.0)
         nc.scalar.activation(out=rstd[:], in_=mean_var[:, :, 1], func=ACT.Sqrt, bias=EPS)
         nc.vector.reciprocal(out=rstd[:], in_=rstd[:])
         for m in range(TOKEN_TILES):

@@ -1,3 +1,4 @@
+import math
 from contextlib import ExitStack
 
 import concourse.mybir as mybir
@@ -18,265 +19,406 @@ FEATURES = 1024
 OUTS = 512
 BASIS = 8
 TOKEN_TILES = TOKENS // P
-OUT_TILES = OUTS // P
-CHUNKS = FEATURES // P
-BASE_PASSES = FEATURES // (P * PACK)
-HALF_OUTS = OUTS // 2
+QUARTER = FEATURES // 4
+ROWS = P // 4
+BLOCKS = 512 // ROWS
+GROUPS = 2
+WIDTH = TOKENS * PACK
+WHOLE = slice(0, WIDTH)
 EPS = 1e-12
 KNOT_STEP = 0.4
 FIRST_KNOT = -2.2
-
-RUN = 4
+KAPPA = math.sqrt(1.0 / 3.0)
 
 FLOPS = 2 * TOKENS * OUTS * (FEATURES + FEATURES * BASIS)
 
 
 def tile_generatorhead_pa_kernel(tc, hidden, base_w1, spline_w1, out):
     nc = tc.nc
-    x_rows = hidden.flatten_outer_dims().rearrange("(m p) i -> p m i", p=P)
-    base_rows = base_w1.rearrange("(n p) i -> p n i", p=P)
-    spline_rows = spline_w1.rearrange("(n p) i c -> p n (i c)", p=P)
+    x_rows = hidden.flatten_outer_dims().rearrange("(n k) (j f) -> (k j) n f", k=ROWS, j=4)
+    base_rows = base_w1.rearrange("(n k) (j f) -> (k j) n f", k=ROWS, j=4)
+    spline_rows = spline_w1.rearrange("(n k) (j f) c -> (k j) n (f c)", k=ROWS, j=4)
     out_rows = out.flatten_outer_dims()
 
     with ExitStack() as ctx:
         keep = ctx.enter_context(tc.tile_pool(name="keep", bufs=1))
-        wload = ctx.enter_context(tc.tile_pool(name="wload", bufs=3))
+        fold = ctx.enter_context(tc.tile_pool(name="fold", bufs=4))
+        once = ctx.enter_context(tc.tile_pool(name="once", bufs=1))
         work = ctx.enter_context(tc.tile_pool(name="work", bufs=2))
-        mx = ctx.enter_context(tc.tile_pool(name="mx", bufs=2))
+        mx = ctx.enter_context(tc.tile_pool(name="mx", bufs=6))
+        wmx = ctx.enter_context(tc.tile_pool(name="wmx", bufs=5))
         acc_pool = ctx.enter_context(tc.psum_pool(name="acc", bufs=1))
-        turn = ctx.enter_context(tc.psum_pool(name="turn", bufs=4))
+        turns = ctx.enter_context(tc.psum_pool(name="turns", bufs=4))
 
-        x_tok = keep.tile([P, TOKEN_TILES, FEATURES], BF16)
-        x_feat = keep.tile([P, CHUNKS, TOKENS], BF16)
-        base_raw = keep.tile([P, OUT_TILES, FEATURES], BF16)
+        x_raw = keep.tile([P, BLOCKS, QUARTER], BF16, tag="raw", name="x_raw")
+        base_raw = keep.tile([P, BLOCKS, QUARTER], BF16, tag="raw", name="base_raw")
+        w_raw = [keep.tile([P, 2, QUARTER * BASIS], BF16, name="w_raw%d" % i) for i in range(BLOCKS // 2)]
+        x_int = keep.tile([P, GROUPS, TOKENS, PACK], BF16)
         acc = [acc_pool.tile([P, OUTS], F32, name="acc%d" % m) for m in range(TOKEN_TILES)]
-        w_raw = {}
         dist = {}
-        neg_w = {}
+        square = {}
         inner = {}
-        outer = {}
+        neg = {}
         side = {}
-        signed = {}
         grouped = {}
         quantised = {}
+        turned = {}
 
-        def load_weights(a):
-            w_raw[a] = wload.tile([P, OUT_TILES, P * BASIS], BF16, name="w_raw")
-            nc.sync.dma_start(out=w_raw[a][:], in_=spline_rows[:, :, a * P * BASIS : (a + 1) * P * BASIS])
+        def turn_bank(source):
+            bank = turns.tile([P, GROUPS, P, 2, 2], BF16, tag="bank", name="bank")
+            for n in range(4):
+                for s in range(2):
+                    nc.tensor.transpose(
+                        bank[:, :, n * ROWS : (n + 1) * ROWS, s, :].rearrange("p q k h -> p k q h"),
+                        source(n, s),
+                        ident[:],
+                    )
+            return bank[:].rearrange("p q k s h -> p q k (s h)")
 
-        def quantise(key, grouped_bf16, width):
-            codes = mx.tile([P, width], U32, align_bytes=64, name=key[0] + "_codes")
-            scales = mx.tile([P, width], U8, align_bytes=64, name=key[0] + "_scales")
-            nc.vector.quantize_mx(out=codes[:].bitcast(FP8X4), scales=scales[:], in_=grouped_bf16)
+        def quantise_act(key, src):
+            codes = mx.tile([P, TOKENS], U32, align_bytes=64, name="act_codes")
+            scales = mx.tile([P, TOKENS], U8, align_bytes=64, name="act_scales")
+            nc.vector.quantize_mx(out=codes[:].bitcast(FP8X4), scales=scales[:], in_=src)
             quantised[key] = (codes, scales)
 
-        def multiply(act_key, w_key, start, stop):
+        def quantise_wide(key):
+            codes = wmx.tile([P, GROUPS * OUTS], U32, align_bytes=64, name="w_codes")
+            scales = wmx.tile([P, GROUPS * OUTS], U8, align_bytes=64, name="w_scales")
+            nc.vector.quantize_mx(
+                out=codes[:].bitcast(FP8X4), scales=scales[:], in_=grouped[key][:].rearrange("p q o t -> p (q o t)")
+            )
+            quantised[key] = (codes, scales)
+
+        def multiply(act_key, act_first, w_key, q, start, stop):
             act_codes, act_scales = quantised[act_key]
             w_codes, w_scales = quantised[w_key]
+            outs = slice(q * OUTS, (q + 1) * OUTS)
             for m in range(TOKEN_TILES):
-                cols = slice(m * P, (m + 1) * P)
+                cols = slice(act_first + m * P, act_first + (m + 1) * P)
                 nc.tensor.matmul_mx(
                     out=acc[m][:],
                     lhsT=act_codes[:, cols].bitcast(FP8X4),
                     lhsT_scale=act_scales[:, cols],
-                    rhs=w_codes[:].bitcast(FP8X4),
-                    rhs_scale=w_scales[:],
+                    rhs=w_codes[:, outs].bitcast(FP8X4),
+                    rhs_scale=w_scales[:, outs],
                     start=start,
                     stop=stop,
                 )
 
-        def distances(a):
-            dist[a] = work.tile([P, PACK, TOKENS], F32, name="dist")
-            for r in range(PACK):
-                nc.scalar.activation(
-                    out=dist[a][:, r, :], in_=x_feat[:, a, :], func=ACT.Abs, scale=1.0 / KNOT_STEP, bias=1.5 - r
-                )
-            nc.scalar.activation(out=dist[a][:], in_=dist[a][:], func=ACT.Abs, bias=-2.0)
+        def turn_weights(source):
+            return [turn_bank(lambda n, s: source(4 * b + n, s)) for b in range(OUTS // P)]
 
-        def clamp(a):
-            neg_w[a] = work.tile([P, PACK, TOKENS], F32, name="neg_w")
-            nc.vector.tensor_scalar(
-                out=neg_w[a][:], in0=dist[a][:], scalar1=2.0, scalar2=2.0, op0=ALU.min, op1=ALU.subtract
-            )
+        def collect_weights(key, banks):
+            grouped[key] = work.tile([P, GROUPS, OUTS, PACK], BF16, align_bytes=64, name="w_grouped")
+            for b in range(OUTS // P):
+                nc.scalar.copy(out=grouped[key][:, :, b * P : (b + 1) * P, :], in_=banks[b])
 
-        def sides(a):
-            side[a] = work.tile([P, PACK, TOKENS], BF16, name="side")
-            for r in range(PACK):
-                nc.vector.tensor_scalar(
-                    out=side[a][:, r, :],
-                    in0=x_feat[:, a, :],
-                    scalar1=FIRST_KNOT + KNOT_STEP * (r + PACK),
-                    scalar2=0.5,
-                    op0=ALU.is_ge,
-                    op1=ALU.subtract,
-                )
+        def spline_source(c):
+            def block(n, s):
+                rows = w_raw[n // 2][:, n % 2, :].rearrange("p (f c) -> p f c", c=BASIS)
+                return rows[:, s * P : (s + 1) * P, c]
 
-        def squares(a):
-            inner[a] = work.tile([P, PACK, TOKENS], F32, name="inner")
-            nc.scalar.activation(out=inner[a][:], in_=neg_w[a][:], func=ACT.Square, bias=2.0)
-            outer[a] = work.tile([P, PACK, TOKENS], F32, name="outer")
-            nc.scalar.activation(out=outer[a][:], in_=neg_w[a][:], func=ACT.Square)
+            return block
 
-        def cubics(a):
-            nc.vector.tensor_tensor(out=inner[a][:], in0=inner[a][:], in1=neg_w[a][:], op=ALU.mult)
-            nc.vector.scalar_tensor_tensor(
-                out=outer[a][:], in0=neg_w[a][:], scalar=-1.0 / 3.0, in1=outer[a][:], op0=ALU.mult, op1=ALU.mult
-            )
-            signed[a] = work.tile([P, PACK, TOKENS], BF16, name="signed")
-            nc.vector.scalar_tensor_tensor(
-                out=signed[a][:], in0=inner[a][:], scalar=4.0 / 3.0, in1=outer[a][:], op0=ALU.add, op1=ALU.min
-            )
-            nc.vector.tensor_tensor(out=signed[a][:], in0=signed[a][:], in1=side[a][:], op=ALU.mult)
-
-        def high_half(a):
-            grouped[a, 1] = work.tile([P, TOKENS, PACK], BF16, align_bytes=64, name="high")
+        def distances(u, part=WHOLE):
+            q, r = u
+            if part.start == 0:
+                dist[u] = fold.tile([P, WIDTH], F32, name="dist")
+            x_flat = x_int[:, q, :, :].rearrange("p k t -> p (k t)")
             nc.scalar.activation(
-                out=grouped[a, 1][:].rearrange("p (c i) r -> p c r i", i=RUN),
-                in_=signed[a][:].rearrange("p r (c i) -> p c r i", i=RUN),
-                func=ACT.Relu,
+                out=dist[u][:, part], in_=x_flat[:, part], func=ACT.Abs, scale=1.0 / KNOT_STEP, bias=1.5 - r
             )
+            nc.scalar.activation(out=dist[u][:, part], in_=dist[u][:, part], func=ACT.Abs, bias=-2.0)
 
-        def low_half(a):
-            grouped[a, 0] = work.tile([P, TOKENS, PACK], BF16, align_bytes=64, name="low")
-            nc.vector.tensor_scalar(
-                out=grouped[a, 0][:].rearrange("p (c i) r -> p c r i", i=RUN),
-                in0=signed[a][:].rearrange("p r (c i) -> p c r i", i=RUN),
-                scalar1=-1.0,
-                scalar2=0.0,
-                op0=ALU.mult,
-                op1=ALU.max,
-            )
-
-        def turn_weights(a):
-            w_words = w_raw[a][:].bitcast(F32).rearrange("p n (f w) -> p n f w", w=BASIS // 2)
-            banks = {}
-            for h in range(2):
-                for half in range(2):
-                    banks[h, half] = turn.tile([P, 2, HALF_OUTS], F32, tag="bank", name="w_bank")
-                    for u in range(2):
-                        for j in range(2):
-                            nc.tensor.transpose(
-                                banks[h, half][:, u, j * P : (j + 1) * P],
-                                w_words[:, 2 * half + j, :, 2 * h + u],
-                                ident_f32[:],
-                            )
-            for h in range(2):
-                grouped["w", a, h] = work.tile([P, OUTS, 2], F32, align_bytes=64, name="w_grouped%d" % h)
-                for half in range(2):
-                    nc.scalar.copy(
-                        out=grouped["w", a, h][:, half * HALF_OUTS : (half + 1) * HALF_OUTS, :],
-                        in_=banks[h, half][:].rearrange("p u o -> p o u"),
-                    )
-
-        def turn_x(pair):
-            x_bank = turn.tile([P, 2, TOKENS], BF16, tag="bank")
-            for j in range(2):
-                a = 2 * pair + j
-                for m in range(TOKEN_TILES):
-                    nc.tensor.transpose(
-                        x_bank[:, j, m * P : (m + 1) * P], x_tok[:, m, a * P : (a + 1) * P], ident_bf[:]
-                    )
-            nc.vector.tensor_copy(out=x_feat[:, 2 * pair : 2 * pair + 2, :], in_=x_bank[:])
-
-        def load_x(pair):
-            cols = slice(2 * pair * P, 2 * (pair + 1) * P)
-            nc.sync.dma_start(out=x_tok[:, :, cols], in_=x_rows[:, :, cols])
-
-        load_x(0)
-        load_x(1)
-        nc.sync.dma_start(out=base_raw[:], in_=base_rows)
-        load_x(2)
-        load_x(3)
-        for a in range(3):
-            load_weights(a)
-
-        ident_bf = keep.tile([P, P], BF16)
-        make_identity(nc, ident_bf[:])
-        ident_f32 = keep.tile([P, P], F32)
-        make_identity(nc, ident_f32[:])
-
-        zero = keep.tile([P, 1], F32)
-        nc.vector.memset(zero[:], 0.0)
-        warm = keep.tile([P, 1], F32)
-        nc.scalar.activation(out=warm[:], in_=zero[:], func=ACT.Silu)
-
-
-        for g in range(BASE_PASSES):
-            turn_x(2 * g)
-            turn_x(2 * g + 1)
-            grouped["base", g] = work.tile([P, OUTS, PACK], BF16, align_bytes=64, name="base_grouped")
-            for half in range(2):
-                base_bank = turn.tile([P, PACK, HALF_OUTS], BF16, tag="bank")
-                for t in range(PACK):
-                    a = PACK * g + t
-                    for j in range(2):
-                        nc.tensor.transpose(
-                            base_bank[:, t, j * P : (j + 1) * P],
-                            base_raw[:, 2 * half + j, a * P : (a + 1) * P],
-                            ident_bf[:],
-                        )
-                nc.vector.tensor_copy(
-                    out=grouped["base", g][:, half * HALF_OUTS : (half + 1) * HALF_OUTS, :],
-                    in_=base_bank[:].rearrange("p t o -> p o t"),
-                )
-        distances(0)
-        clamp(0)
-        sides(0)
-        for g in range(BASE_PASSES):
-            quantise(("base", g), grouped["base", g][:].rearrange("p o t -> p (o t)"), OUTS)
-        for g in range(BASE_PASSES):
-            grouped["silu", g] = work.tile([P, TOKENS, PACK], BF16, align_bytes=64, name="silu_grouped")
+        def squares(u, part=WHOLE):
+            if part.start == 0:
+                square[u] = fold.tile([P, WIDTH], F32, name="square")
             nc.scalar.activation(
-                out=grouped["silu", g][:].rearrange("p (c i) t -> p c t i", i=RUN),
-                in_=x_feat[:, PACK * g : PACK * (g + 1), :].rearrange("p t (c i) -> p c t i", i=RUN),
-                func=ACT.Silu,
+                out=square[u][:, part], in_=dist[u][:, part], func=ACT.Square, scale=-KAPPA, bias=2.0 * KAPPA
             )
-        squares(0)
-        distances(1)
-        turn_weights(0)
-        for g in range(BASE_PASSES):
-            quantise(("silu", g), grouped["silu", g][:].rearrange("p k t -> p (k t)"), TOKENS)
-            multiply(("silu", g), ("base", g), start=(g == 0), stop=False)
 
-        for a in range(CHUNKS):
-            cubics(a)
-            high_half(a)
-            if a + 1 < CHUNKS:
-                clamp(a + 1)
-                squares(a + 1)
-            low_half(a)
-            if a + 1 < CHUNKS:
-                sides(a + 1)
-            if a + 2 < CHUNKS:
-                distances(a + 2)
-            if a + 3 < CHUNKS:
-                load_weights(a + 3)
-            if a + 1 < CHUNKS:
-                turn_weights(a + 1)
-            for h in range(2):
-                quantise(("basis", a, h), grouped[a, h][:].rearrange("p k t -> p (k t)"), TOKENS)
-                quantise(("spline", a, h), grouped["w", a, h][:].rearrange("p o u -> p (o u)").bitcast(BF16), OUTS)
-                multiply(("basis", a, h), ("spline", a, h), start=False, stop=(a == CHUNKS - 1 and h == 1))
+        def partner(u):
+            return (u[0], (u[1] + 2) % PACK)
 
-        nc.scalar.activation(out=warm[:], in_=grouped[CHUNKS - 1, 1][:, 0, 0:1], func=ACT.Gelu)
-        stats = keep.tile([P, TOKEN_TILES, 6], F32)
-        mean_var = keep.tile([P, TOKEN_TILES, 2], F32)
-        rstd = keep.tile([P, TOKEN_TILES], F32)
-        gelu = [keep.tile([P, OUTS], F32, name="gelu%d" % m) for m in range(TOKEN_TILES)]
-        for m in range(TOKEN_TILES):
-            nc.scalar.activation(out=gelu[m][:], in_=acc[m][:], func=ACT.Gelu)
-            nc.vector.bn_stats(out=stats[:, m, :], in_=gelu[m][:])
-            nc.vector.bn_aggr(out=mean_var[:, m, :], in_=stats[:, m, :])
-        nc.scalar.activation(out=warm[:], in_=gelu[TOKEN_TILES - 1][:, 0:1], func=ACT.Sqrt, scale=0.0)
-        nc.scalar.activation(out=rstd[:], in_=mean_var[:, :, 1], func=ACT.Sqrt, bias=EPS)
-        nc.vector.reciprocal(out=rstd[:], in_=rstd[:])
-        for m in range(TOKEN_TILES):
-            nc.vector.tensor_scalar(
-                out=gelu[m][:],
-                in0=gelu[m][:],
-                scalar1=mean_var[:, m, 0:1],
-                scalar2=rstd[:, m : m + 1],
+        def outer_piece(u, part=WHOLE):
+            if part.start == 0:
+                neg[u] = work.tile([P, WIDTH], BF16, name="neg")
+            nc.vector.scalar_tensor_tensor(
+                out=neg[u][:, part],
+                in0=dist[u][:, part],
+                scalar=2.0,
+                in1=square[u][:, part],
                 op0=ALU.subtract,
                 op1=ALU.mult,
             )
-            nc.sync.dma_start(out=out_rows[m * P : (m + 1) * P, :], in_=gelu[m][:])
+
+        def inner_product(u, part=WHOLE):
+            other = square[partner(u)]
+            nc.vector.scalar_tensor_tensor(
+                out=other[:, part],
+                in0=dist[u][:, part],
+                scalar=2.0,
+                in1=other[:, part],
+                op0=ALU.subtract,
+                op1=ALU.mult,
+            )
+
+        def inner_piece(u, on_scalar):
+            inner[u] = work.tile([P, WIDTH], BF16, name="inner")
+            product = square[partner(u)]
+            if on_scalar:
+                nc.scalar.activation(
+                    out=inner[u][:], in_=product[:], func=ACT.Identity, scale=-3.0, bias=-4.0 / 3.0
+                )
+            else:
+                nc.vector.tensor_scalar(
+                    out=inner[u][:], in0=product[:], scalar1=-3.0, scalar2=-4.0 / 3.0, op0=ALU.mult, op1=ALU.add
+                )
+
+        def sides(u):
+            q, r = u
+            side[u] = once.tile([P, WIDTH], BF16, name="side")
+            nc.vector.tensor_scalar(
+                out=side[u][:],
+                in0=x_int[:, q, :, :].rearrange("p k t -> p (k t)"),
+                scalar1=FIRST_KNOT + KNOT_STEP * (r + PACK),
+                scalar2=0.5,
+                op0=ALU.is_ge,
+                op1=ALU.subtract,
+            )
+
+        def join(u):
+            nc.vector.tensor_tensor(out=neg[u][:], in0=neg[u][:], in1=inner[u][:], op=ALU.max)
+
+        def clip(u):
+            nc.vector.tensor_scalar_min(out=neg[u][:], in0=neg[u][:], scalar1=0.0)
+
+        def sign(u):
+            nc.vector.tensor_tensor(out=neg[u][:], in0=neg[u][:], in1=side[u][:], op=ALU.mult)
+
+        def split(u):
+            q, r = u
+            grouped["basis", q, r] = once.tile([P, WIDTH], BF16, align_bytes=64, name="low")
+            grouped["basis", q, r + PACK] = once.tile([P, WIDTH], BF16, align_bytes=64, name="high")
+            nc.vector.tensor_scalar(
+                out=grouped["basis", q, r + PACK][:], in0=neg[u][:], scalar1=-1.0, scalar2=0.0, op0=ALU.mult, op1=ALU.max
+            )
+            nc.vector.tensor_scalar_max(out=grouped["basis", q, r][:], in0=neg[u][:], scalar1=0.0)
+
+        def quantise_unit(u):
+            q, r = u
+            for c in (r + PACK, r):
+                quantise_act(("basis", q, c), grouped["basis", q, c][:])
+
+        def contract(u):
+            q, r = u
+            for c in (r + PACK, r):
+                multiply(
+                    ("basis", q, c),
+                    0,
+                    ("spline", c),
+                    q,
+                    start=(u == units[0] and c == r + PACK),
+                    stop=(u == units[len(units) - 1] and c == r),
+                )
+
+        def turn(c):
+            turned[c] = turn_weights(spline_source(c))
+
+        def collect(c):
+            collect_weights(("spline", c), turned[c])
+
+        for b in range(TOKEN_TILES):
+            nc.sync.dma_start(out=x_raw[:, 4 * b : 4 * b + 4, :], in_=x_rows[:, 4 * b : 4 * b + 4, :])
+        for i in range(BLOCKS // 2):
+            nc.sync.dma_start(out=w_raw[i][:], in_=spline_rows[:, 2 * i : 2 * i + 2, :])
+
+        ident = keep.tile([P, P], BF16)
+        make_identity(nc, ident[:])
+        zero = keep.tile([P, 1], F32)
+        nc.vector.memset(zero[:], 0.0)
+        minus_half = keep.tile([P, 1], F32)
+        nc.gpsimd.memset(minus_half[:], -0.5)
+        warm = keep.tile([P, 1], F32)
+        nc.scalar.activation(out=warm[:], in_=zero[:], func=ACT.Silu)
+
+        pairs = [((q, r), (q, r + 2)) for r in range(2) for q in range(GROUPS)]
+        units = [u for pair in pairs for u in pair]
+        quarters = [slice(b * P * PACK, (b + 1) * P * PACK) for b in range(TOKEN_TILES)]
+
+        def products(a, b, part):
+            outer_piece(b, part)
+            inner_product(a, part)
+            outer_piece(a, part)
+            inner_product(b, part)
+
+        with tc.manual_schedule():
+            for b in range(TOKEN_TILES):
+                nc.vector.tensor_copy(
+                    out=x_int[:, :, b * P : (b + 1) * P, :],
+                    in_=turn_bank(lambda n, s: x_raw[:, 4 * b + n, s * P : (s + 1) * P]),
+                )
+            nc.sync.dma_start(out=base_raw[:], in_=base_rows)
+            for part in quarters:
+                for u in (pairs[0][1], pairs[0][0]):
+                    distances(u, part)
+                    squares(u, part)
+                products(*pairs[0], part)
+
+            a, b = pairs[0]
+            a1, b1 = pairs[1]
+            turn(4)
+            distances(b1)
+            squares(b1)
+            inner_piece(a, False)
+            sides(a)
+            join(a)
+            inner_piece(b, False)
+            clip(a)
+            join(b)
+            sign(a)
+            collect(4)
+            turn(0)
+            clip(b)
+            split(a)
+            sides(b)
+            quantise_unit(a)
+            distances(a1)
+            collect(0)
+            turn(6)
+            squares(a1)
+            sign(b)
+            quantise_wide(("spline", 4))
+            split(b)
+            collect(6)
+            turn(2)
+
+            before = b
+            a, b = a1, b1
+            a1, b1 = pairs[2]
+            outer_piece(b)
+            quantise_unit(before)
+            inner_product(a)
+            quantise_wide(("spline", 0))
+            distances(b1)
+            inner_piece(a, True)
+            outer_piece(a)
+            collect(2)
+            turn(5)
+            inner_product(b)
+            squares(b1)
+            sides(a)
+            inner_piece(b, False)
+            join(a)
+            quantise_wide(("spline", 6))
+            contract(units[0])
+            clip(a)
+            join(b)
+            sign(a)
+            quantise_wide(("spline", 2))
+            contract(before)
+            clip(b)
+            collect(5)
+            turn(1)
+            split(a)
+            sides(b)
+            distances(a1)
+            quantise_unit(a)
+            contract(a)
+            sign(b)
+            squares(a1)
+            split(b)
+
+            before = b
+            a, b = a1, b1
+            a1, b1 = pairs[3]
+            outer_piece(b)
+            quantise_unit(before)
+            contract(before)
+            collect(1)
+            turn(7)
+            inner_product(a)
+            quantise_wide(("spline", 5))
+            distances(b1)
+            inner_piece(a, True)
+            outer_piece(a)
+            inner_product(b)
+            squares(b1)
+            sides(a)
+            inner_piece(b, False)
+            join(a)
+            quantise_wide(("spline", 1))
+            clip(a)
+            join(b)
+            sign(a)
+            collect(7)
+            turn(3)
+            clip(b)
+            split(a)
+            sides(b)
+            distances(a1)
+            quantise_unit(a)
+            contract(a)
+            sign(b)
+            quantise_wide(("spline", 7))
+            squares(a1)
+            split(b)
+            collect(3)
+            base_banks = turn_weights(lambda n, s: base_raw[:, n, s * P : (s + 1) * P])
+
+            before = b
+            a, b = a1, b1
+            outer_piece(b)
+            quantise_unit(before)
+            inner_product(a)
+            quantise_wide(("spline", 3))
+            contract(before)
+            inner_piece(a, True)
+            outer_piece(a)
+            collect_weights(("base",), base_banks)
+            inner_product(b)
+            inner_piece(b, True)
+            sides(a)
+            join(a)
+            quantise_wide(("base",))
+            clip(a)
+            join(b)
+            grouped["silu"] = work.tile(
+                [P, GROUPS, TOKENS, PACK], BF16, align_bytes=64, tag="w_grouped", name="silu"
+            )
+            nc.scalar.activation(out=grouped["silu"][:], in_=x_int[:], func=ACT.Silu)
+            sign(a)
+            clip(b)
+            split(a)
+            sides(b)
+            quantise_unit(a)
+            contract(a)
+            quantise_wide("silu")
+            for q in range(GROUPS):
+                multiply("silu", q * TOKENS, ("base",), q, start=False, stop=False)
+            sign(b)
+            split(b)
+            quantise_unit(b)
+            contract(b)
+
+            nc.scalar.activation(out=warm[:], in_=zero[:], func=ACT.Gelu)
+            stats = keep.tile([P, TOKEN_TILES, 6], F32)
+            mean_var = keep.tile([P, TOKEN_TILES, 2], F32)
+            rstd = keep.tile([P, TOKEN_TILES], F32)
+            gelu = fold.tile([P, TOKEN_TILES, OUTS], F32, tag="dist", name="gelu")
+            for m in range(TOKEN_TILES):
+                nc.scalar.activation(out=gelu[:, m, :], in_=acc[m][:], func=ACT.Gelu)
+                nc.vector.bn_stats(out=stats[:, m, :], in_=gelu[:, m, :])
+                nc.vector.bn_aggr(out=mean_var[:, m, :], in_=stats[:, m, :])
+                nc.vector.tensor_scalar_add(out=mean_var[:, m, 1:2], in0=mean_var[:, m, 1:2], scalar1=EPS)
+                nc.gpsimd.tensor_tensor(out=rstd[:, m : m + 1], in0=mean_var[:, m, 1:2], in1=minus_half[:], op=ALU.pow)
+            for m in range(TOKEN_TILES):
+                nc.vector.tensor_scalar(
+                    out=gelu[:, m, :],
+                    in0=gelu[:, m, :],
+                    scalar1=mean_var[:, m, 0:1],
+                    scalar2=rstd[:, m : m + 1],
+                    op0=ALU.subtract,
+                    op1=ALU.mult,
+                )
+                nc.sync.dma_start(out=out_rows[m * P : (m + 1) * P, :], in_=gelu[:, m, :])

@@ -73,13 +73,16 @@ def tile_generatorhead_pa_kernel(tc, hidden, base_w1, spline_w1, out):
                         source(n, s),
                         ident[:],
                     )
-            return bank[:].rearrange("p q k s h -> p q k (s h)")
+            return bank
 
-        def quantise_act(key, src):
-            codes = mx.tile([P, TOKENS], U32, align_bytes=64, name="act_codes")
-            scales = mx.tile([P, TOKENS], U8, align_bytes=64, name="act_scales")
-            nc.vector.quantize_mx(out=codes[:].bitcast(FP8X4), scales=scales[:], in_=src)
-            quantised[key] = (codes, scales)
+        def quantise_act(key, src, part):
+            if part.start == 0:
+                codes = mx.tile([P, TOKENS], U32, align_bytes=64, name="act_codes")
+                scales = mx.tile([P, TOKENS], U8, align_bytes=64, name="act_scales")
+                quantised[key] = (codes, scales)
+            codes, scales = quantised[key]
+            words = slice(part.start // PACK, part.stop // PACK)
+            nc.vector.quantize_mx(out=codes[:, words].bitcast(FP8X4), scales=scales[:, words], in_=src[:, part])
 
         def quantise_wide(key):
             codes = wmx.tile([P, GROUPS * OUTS], U32, align_bytes=64, name="w_codes")
@@ -89,11 +92,11 @@ def tile_generatorhead_pa_kernel(tc, hidden, base_w1, spline_w1, out):
             )
             quantised[key] = (codes, scales)
 
-        def multiply(act_key, act_first, w_key, q, start, stop):
+        def multiply(act_key, act_first, w_key, q, start, stop, tiles=range(TOKEN_TILES)):
             act_codes, act_scales = quantised[act_key]
             w_codes, w_scales = quantised[w_key]
             outs = slice(q * OUTS, (q + 1) * OUTS)
-            for m in range(TOKEN_TILES):
+            for m in tiles:
                 cols = slice(act_first + m * P, act_first + (m + 1) * P)
                 nc.tensor.matmul_mx(
                     out=acc[m][:],
@@ -111,7 +114,10 @@ def tile_generatorhead_pa_kernel(tc, hidden, base_w1, spline_w1, out):
         def collect_weights(key, banks):
             grouped[key] = work.tile([P, GROUPS, OUTS, PACK], BF16, align_bytes=64, name="w_grouped")
             for b in range(OUTS // P):
-                nc.scalar.copy(out=grouped[key][:, :, b * P : (b + 1) * P, :], in_=banks[b])
+                rows = grouped[key][:, :, b * P : (b + 1) * P, :].rearrange("p q k t -> p q (k t)")
+                nc.scalar.copy(
+                    out=rows.bitcast(F32), in_=banks[b][:].rearrange("p q k s h -> p q (k s h)").bitcast(F32)
+                )
 
         def spline_source(c):
             def block(n, s):
@@ -163,21 +169,22 @@ def tile_generatorhead_pa_kernel(tc, hidden, base_w1, spline_w1, out):
                 op1=ALU.mult,
             )
 
-        def inner_piece(u, on_scalar):
-            inner[u] = work.tile([P, WIDTH], BF16, name="inner")
-            product = square[partner(u)]
+        def inner_piece(u, on_scalar, part=WHOLE):
+            if part.start == 0:
+                inner[u] = work.tile([P, WIDTH], BF16, name="inner")
+            source = square[partner(u)][:, part]
             if on_scalar:
                 nc.scalar.activation(
-                    out=inner[u][:], in_=product[:], func=ACT.Identity, scale=-3.0, bias=-4.0 / 3.0
+                    out=inner[u][:, part], in_=source, func=ACT.Identity, scale=-3.0, bias=-4.0 / 3.0
                 )
             else:
                 nc.vector.tensor_scalar(
-                    out=inner[u][:], in0=product[:], scalar1=-3.0, scalar2=-4.0 / 3.0, op0=ALU.mult, op1=ALU.add
+                    out=inner[u][:, part], in0=source, scalar1=-3.0, scalar2=-4.0 / 3.0, op0=ALU.mult, op1=ALU.add
                 )
 
         def sides(u):
             q, r = u
-            side[u] = once.tile([P, WIDTH], BF16, name="side")
+            side[u] = work.tile([P, WIDTH], BF16, name="side")
             nc.vector.tensor_scalar(
                 out=side[u][:],
                 in0=x_int[:, q, :, :].rearrange("p k t -> p (k t)"),
@@ -187,30 +194,39 @@ def tile_generatorhead_pa_kernel(tc, hidden, base_w1, spline_w1, out):
                 op1=ALU.subtract,
             )
 
-        def join(u):
-            nc.vector.tensor_tensor(out=neg[u][:], in0=neg[u][:], in1=inner[u][:], op=ALU.max)
+        def join(u, part=WHOLE):
+            values = neg[u][:, part]
+            nc.vector.tensor_tensor(out=values, in0=values, in1=inner[u][:, part], op=ALU.max)
 
-        def clip(u):
-            nc.vector.tensor_scalar_min(out=neg[u][:], in0=neg[u][:], scalar1=0.0)
+        def clip(u, part=WHOLE):
+            values = neg[u][:, part]
+            nc.vector.tensor_scalar_min(out=values, in0=values, scalar1=0.0)
 
-        def sign(u):
-            nc.vector.tensor_tensor(out=neg[u][:], in0=neg[u][:], in1=side[u][:], op=ALU.mult)
+        def sign(u, part=WHOLE):
+            values = neg[u][:, part]
+            nc.vector.tensor_tensor(out=values, in0=values, in1=side[u][:, part], op=ALU.mult)
 
-        def split(u):
+        def split(u, part=WHOLE):
             q, r = u
-            grouped["basis", q, r] = once.tile([P, WIDTH], BF16, align_bytes=64, name="low")
-            grouped["basis", q, r + PACK] = once.tile([P, WIDTH], BF16, align_bytes=64, name="high")
+            if part.start == 0:
+                grouped["basis", q, r] = once.tile([P, WIDTH], BF16, align_bytes=64, name="low")
+                grouped["basis", q, r + PACK] = once.tile([P, WIDTH], BF16, align_bytes=64, name="high")
             nc.vector.tensor_scalar(
-                out=grouped["basis", q, r + PACK][:], in0=neg[u][:], scalar1=-1.0, scalar2=0.0, op0=ALU.mult, op1=ALU.max
+                out=grouped["basis", q, r + PACK][:, part],
+                in0=neg[u][:, part],
+                scalar1=-1.0,
+                scalar2=0.0,
+                op0=ALU.mult,
+                op1=ALU.max,
             )
-            nc.vector.tensor_scalar_max(out=grouped["basis", q, r][:], in0=neg[u][:], scalar1=0.0)
+            nc.vector.tensor_scalar_max(out=grouped["basis", q, r][:, part], in0=neg[u][:, part], scalar1=0.0)
 
-        def quantise_unit(u):
+        def quantise_unit(u, part=WHOLE):
             q, r = u
             for c in (r + PACK, r):
-                quantise_act(("basis", q, c), grouped["basis", q, c][:])
+                quantise_act(("basis", q, c), grouped["basis", q, c], part)
 
-        def contract(u):
+        def contract(u, tiles=range(TOKEN_TILES)):
             q, r = u
             for c in (r + PACK, r):
                 multiply(
@@ -220,6 +236,7 @@ def tile_generatorhead_pa_kernel(tc, hidden, base_w1, spline_w1, out):
                     q,
                     start=(u == units[0] and c == r + PACK),
                     stop=(u == units[len(units) - 1] and c == r),
+                    tiles=tiles,
                 )
 
         def turn(c):
@@ -237,13 +254,14 @@ def tile_generatorhead_pa_kernel(tc, hidden, base_w1, spline_w1, out):
         make_identity(nc, ident[:])
         zero = keep.tile([P, 1], F32)
         nc.vector.memset(zero[:], 0.0)
-        minus_half = keep.tile([P, 1], F32)
+        minus_half = keep.tile([P, TOKEN_TILES], F32)
         nc.gpsimd.memset(minus_half[:], -0.5)
         warm = keep.tile([P, 1], F32)
         nc.scalar.activation(out=warm[:], in_=zero[:], func=ACT.Silu)
 
         pairs = [((q, r), (q, r + 2)) for r in range(2) for q in range(GROUPS)]
         units = [u for pair in pairs for u in pair]
+        halves = [slice(0, WIDTH // 2), slice(WIDTH // 2, WIDTH)]
         quarters = [slice(b * P * PACK, (b + 1) * P * PACK) for b in range(TOKEN_TILES)]
 
         def products(a, b, part):
@@ -256,7 +274,9 @@ def tile_generatorhead_pa_kernel(tc, hidden, base_w1, spline_w1, out):
             for b in range(TOKEN_TILES):
                 nc.vector.tensor_copy(
                     out=x_int[:, :, b * P : (b + 1) * P, :],
-                    in_=turn_bank(lambda n, s: x_raw[:, 4 * b + n, s * P : (s + 1) * P]),
+                    in_=turn_bank(lambda n, s: x_raw[:, 4 * b + n, s * P : (s + 1) * P])[:].rearrange(
+                        "p q k s h -> p q k (s h)"
+                    ),
                 )
             nc.sync.dma_start(out=base_raw[:], in_=base_rows)
             for part in quarters:
@@ -264,30 +284,36 @@ def tile_generatorhead_pa_kernel(tc, hidden, base_w1, spline_w1, out):
                     distances(u, part)
                     squares(u, part)
                 products(*pairs[0], part)
+                if part.start == 0:
+                    sides(pairs[0][0])
+                if part == quarters[1]:
+                    sides(pairs[0][1])
+                    inner_piece(pairs[0][0], False, halves[0])
+                if part == quarters[2]:
+                    inner_piece(pairs[0][1], False, halves[0])
+                    join(pairs[0][0], halves[0])
 
             a, b = pairs[0]
             a1, b1 = pairs[1]
             turn(4)
             distances(b1)
             squares(b1)
-            inner_piece(a, False)
-            sides(a)
-            join(a)
-            inner_piece(b, False)
-            clip(a)
+            inner_piece(a, False, halves[1])
+            inner_piece(b, False, halves[1])
+            join(a, halves[1])
             join(b)
+            clip(a)
+            clip(b)
             sign(a)
             collect(4)
             turn(0)
-            clip(b)
+            sign(b)
             split(a)
-            sides(b)
             quantise_unit(a)
             distances(a1)
             collect(0)
             turn(6)
             squares(a1)
-            sign(b)
             quantise_wide(("spline", 4))
             split(b)
             collect(6)
@@ -301,10 +327,10 @@ def tile_generatorhead_pa_kernel(tc, hidden, base_w1, spline_w1, out):
             inner_product(a)
             quantise_wide(("spline", 0))
             distances(b1)
-            inner_piece(a, True)
             outer_piece(a)
             collect(2)
             turn(5)
+            inner_piece(a, False)
             inner_product(b)
             squares(b1)
             sides(a)
@@ -345,7 +371,7 @@ def tile_generatorhead_pa_kernel(tc, hidden, base_w1, spline_w1, out):
             inner_product(b)
             squares(b1)
             sides(a)
-            inner_piece(b, False)
+            inner_piece(b, True)
             join(a)
             quantise_wide(("spline", 1))
             clip(a)
@@ -379,46 +405,61 @@ def tile_generatorhead_pa_kernel(tc, hidden, base_w1, spline_w1, out):
             inner_product(b)
             inner_piece(b, True)
             sides(a)
+            sides(b)
             join(a)
             quantise_wide(("base",))
             clip(a)
-            join(b)
             grouped["silu"] = work.tile(
                 [P, GROUPS, TOKENS, PACK], BF16, align_bytes=64, tag="w_grouped", name="silu"
             )
             nc.scalar.activation(out=grouped["silu"][:], in_=x_int[:], func=ACT.Silu)
             sign(a)
-            clip(b)
+            join(b, halves[0])
             split(a)
-            sides(b)
+            clip(b, halves[0])
             quantise_unit(a)
             contract(a)
+            sign(b, halves[0])
             quantise_wide("silu")
             for q in range(GROUPS):
                 multiply("silu", q * TOKENS, ("base",), q, start=False, stop=False)
-            sign(b)
-            split(b)
-            quantise_unit(b)
-            contract(b)
+            split(b, halves[0])
+            join(b, halves[1])
+            quantise_unit(b, halves[0])
+            contract(b, (0, 1))
+            clip(b, halves[1])
+            sign(b, halves[1])
+            split(b, halves[1])
+            quantise_unit(b, halves[1])
+            contract(b, (2, 3))
 
             nc.scalar.activation(out=warm[:], in_=zero[:], func=ACT.Gelu)
             stats = keep.tile([P, TOKEN_TILES, 6], F32)
             mean_var = keep.tile([P, TOKEN_TILES, 2], F32)
             rstd = keep.tile([P, TOKEN_TILES], F32)
             gelu = fold.tile([P, TOKEN_TILES, OUTS], F32, tag="dist", name="gelu")
-            for m in range(TOKEN_TILES):
-                nc.scalar.activation(out=gelu[:, m, :], in_=acc[m][:], func=ACT.Gelu)
-                nc.vector.bn_stats(out=stats[:, m, :], in_=gelu[:, m, :])
-                nc.vector.bn_aggr(out=mean_var[:, m, :], in_=stats[:, m, :])
-                nc.vector.tensor_scalar_add(out=mean_var[:, m, 1:2], in0=mean_var[:, m, 1:2], scalar1=EPS)
-                nc.gpsimd.tensor_tensor(out=rstd[:, m : m + 1], in0=mean_var[:, m, 1:2], in1=minus_half[:], op=ALU.pow)
-            for m in range(TOKEN_TILES):
-                nc.vector.tensor_scalar(
-                    out=gelu[:, m, :],
-                    in0=gelu[:, m, :],
-                    scalar1=mean_var[:, m, 0:1],
-                    scalar2=rstd[:, m : m + 1],
-                    op0=ALU.subtract,
-                    op1=ALU.mult,
+            for h in range(2):
+                tiles = (2 * h, 2 * h + 1)
+                for m in tiles:
+                    nc.scalar.activation(out=gelu[:, m, :], in_=acc[m][:], func=ACT.Gelu)
+                for m in tiles:
+                    nc.vector.bn_stats(out=stats[:, m, :], in_=gelu[:, m, :])
+                for m in tiles:
+                    nc.vector.bn_aggr(out=mean_var[:, m, :], in_=stats[:, m, :])
+                columns = slice(2 * h, 2 * h + 2)
+                nc.gpsimd.tensor_scalar(
+                    out=rstd[:, columns], in0=mean_var[:, columns, 1], scalar1=EPS, scalar2=0.0, op0=ALU.add, op1=ALU.add
                 )
-                nc.sync.dma_start(out=out_rows[m * P : (m + 1) * P, :], in_=gelu[:, m, :])
+                nc.gpsimd.tensor_tensor(
+                    out=rstd[:, columns], in0=rstd[:, columns], in1=minus_half[:, columns], op=ALU.pow
+                )
+                for m in tiles:
+                    nc.vector.tensor_scalar(
+                        out=gelu[:, m, :],
+                        in0=gelu[:, m, :],
+                        scalar1=mean_var[:, m, 0:1],
+                        scalar2=rstd[:, m : m + 1],
+                        op0=ALU.subtract,
+                        op1=ALU.mult,
+                    )
+                    nc.sync.dma_start(out=out_rows[m * P : (m + 1) * P, :], in_=gelu[:, m, :])

@@ -42,10 +42,11 @@ def tile_generatorhead_pa_kernel(tc, hidden, base_w1, spline_w1, out):
 
     with ExitStack() as ctx:
         keep = ctx.enter_context(tc.tile_pool(name="keep", bufs=1))
-        fold = ctx.enter_context(tc.tile_pool(name="fold", bufs=4))
+        fold = ctx.enter_context(tc.tile_pool(name="fold", bufs=3))
         once = ctx.enter_context(tc.tile_pool(name="once", bufs=1))
         work = ctx.enter_context(tc.tile_pool(name="work", bufs=2))
-        mx = ctx.enter_context(tc.tile_pool(name="mx", bufs=6))
+        sided = ctx.enter_context(tc.tile_pool(name="sided", bufs=6))
+        mx = ctx.enter_context(tc.tile_pool(name="mx", bufs=7))
         wmx = ctx.enter_context(tc.tile_pool(name="wmx", bufs=5))
         acc_pool = ctx.enter_context(tc.psum_pool(name="acc", bufs=1))
         turns = ctx.enter_context(tc.psum_pool(name="turns", bufs=4))
@@ -81,8 +82,9 @@ def tile_generatorhead_pa_kernel(tc, hidden, base_w1, spline_w1, out):
                 scales = mx.tile([P, TOKENS], U8, align_bytes=64, name="act_scales")
                 quantised[key] = (codes, scales)
             codes, scales = quantised[key]
-            words = slice(part.start // PACK, part.stop // PACK)
-            nc.vector.quantize_mx(out=codes[:, words].bitcast(FP8X4), scales=scales[:, words], in_=src[:, part])
+            for piece in (halves[0], quarters[2]) if part == most else (part,):
+                words = slice(piece.start // PACK, piece.stop // PACK)
+                nc.vector.quantize_mx(out=codes[:, words].bitcast(FP8X4), scales=scales[:, words], in_=src[:, piece])
 
         def quantise_wide(key):
             codes = wmx.tile([P, GROUPS * OUTS], U32, align_bytes=64, name="w_codes")
@@ -126,7 +128,7 @@ def tile_generatorhead_pa_kernel(tc, hidden, base_w1, spline_w1, out):
 
             return block
 
-        def distances(u, part=WHOLE):
+        def first_fold(u, part=WHOLE):
             q, r = u
             if part.start == 0:
                 dist[u] = fold.tile([P, WIDTH], F32, name="dist")
@@ -134,7 +136,13 @@ def tile_generatorhead_pa_kernel(tc, hidden, base_w1, spline_w1, out):
             nc.scalar.activation(
                 out=dist[u][:, part], in_=x_flat[:, part], func=ACT.Abs, scale=1.0 / KNOT_STEP, bias=1.5 - r
             )
+
+        def refold(u, part=WHOLE):
             nc.scalar.activation(out=dist[u][:, part], in_=dist[u][:, part], func=ACT.Abs, bias=-2.0)
+
+        def distances(u):
+            first_fold(u)
+            refold(u)
 
         def squares(u, part=WHOLE):
             if part.start == 0:
@@ -184,7 +192,7 @@ def tile_generatorhead_pa_kernel(tc, hidden, base_w1, spline_w1, out):
 
         def sides(u):
             q, r = u
-            side[u] = work.tile([P, WIDTH], BF16, name="side")
+            side[u] = sided.tile([P, WIDTH], BF16, name="side")
             nc.vector.tensor_scalar(
                 out=side[u][:],
                 in0=x_int[:, q, :, :].rearrange("p k t -> p (k t)"),
@@ -262,7 +270,9 @@ def tile_generatorhead_pa_kernel(tc, hidden, base_w1, spline_w1, out):
         pairs = [((q, r), (q, r + 2)) for r in range(2) for q in range(GROUPS)]
         units = [u for pair in pairs for u in pair]
         halves = [slice(0, WIDTH // 2), slice(WIDTH // 2, WIDTH)]
+        most, rest = slice(0, 3 * WIDTH // 4), slice(3 * WIDTH // 4, WIDTH)
         quarters = [slice(b * P * PACK, (b + 1) * P * PACK) for b in range(TOKEN_TILES)]
+        steps = [slice(0, WIDTH // 4), slice(WIDTH // 4, WIDTH // 2), halves[1]]
 
         def products(a, b, part):
             outer_piece(b, part)
@@ -279,25 +289,30 @@ def tile_generatorhead_pa_kernel(tc, hidden, base_w1, spline_w1, out):
                     ),
                 )
             nc.sync.dma_start(out=base_raw[:], in_=base_rows)
-            for part in quarters:
-                for u in (pairs[0][1], pairs[0][0]):
-                    distances(u, part)
-                    squares(u, part)
-                products(*pairs[0], part)
-                if part.start == 0:
-                    sides(pairs[0][0])
-                if part == quarters[1]:
-                    sides(pairs[0][1])
-                    inner_piece(pairs[0][0], False, halves[0])
-                if part == quarters[2]:
-                    inner_piece(pairs[0][1], False, halves[0])
-                    join(pairs[0][0], halves[0])
-
             a, b = pairs[0]
             a1, b1 = pairs[1]
+            for part in steps:
+                first_fold(b, part)
+                first_fold(a, part)
+                refold(b, part)
+                refold(a, part)
+                squares(b, part)
+                squares(a, part)
+                products(a, b, part)
+                if part == steps[0]:
+                    sides(a)
+                    sides(b)
+                    sides(a1)
+                if part == steps[1]:
+                    sides(b1)
+                    sides(pairs[2][0])
+                    inner_piece(a, False, halves[0])
+                    join(a, halves[0])
+
             turn(4)
             distances(b1)
             squares(b1)
+            inner_piece(b, False, halves[0])
             inner_piece(a, False, halves[1])
             inner_piece(b, False, halves[1])
             join(a, halves[1])
@@ -311,13 +326,11 @@ def tile_generatorhead_pa_kernel(tc, hidden, base_w1, spline_w1, out):
             split(a)
             quantise_unit(a)
             distances(a1)
+            squares(a1)
             collect(0)
             turn(6)
-            squares(a1)
             quantise_wide(("spline", 4))
             split(b)
-            collect(6)
-            turn(2)
 
             before = b
             a, b = a1, b1
@@ -325,33 +338,36 @@ def tile_generatorhead_pa_kernel(tc, hidden, base_w1, spline_w1, out):
             outer_piece(b)
             quantise_unit(before)
             inner_product(a)
+            first_fold(b1)
+            inner_piece(a, True)
             quantise_wide(("spline", 0))
-            distances(b1)
-            outer_piece(a)
-            collect(2)
-            turn(5)
-            inner_piece(a, False)
-            inner_product(b)
-            squares(b1)
-            sides(a)
-            inner_piece(b, False)
-            join(a)
-            quantise_wide(("spline", 6))
             contract(units[0])
+            outer_piece(a)
+            inner_product(b)
+            refold(b1)
+            inner_piece(b, True)
+            collect(6)
+            turn(2)
+            join(a)
+            sides(b1)
+            squares(b1)
             clip(a)
             join(b)
             sign(a)
-            quantise_wide(("spline", 2))
-            contract(before)
-            clip(b)
-            collect(5)
-            turn(1)
+            quantise_wide(("spline", 6))
+            collect(2)
+            turn(5)
             split(a)
-            sides(b)
-            distances(a1)
+            clip(b)
+            first_fold(a1)
             quantise_unit(a)
             contract(a)
+            collect(5)
+            turn(1)
             sign(b)
+            quantise_wide(("spline", 2))
+            contract(before)
+            refold(a1)
             squares(a1)
             split(b)
 
@@ -361,92 +377,91 @@ def tile_generatorhead_pa_kernel(tc, hidden, base_w1, spline_w1, out):
             outer_piece(b)
             quantise_unit(before)
             contract(before)
-            collect(1)
-            turn(7)
             inner_product(a)
-            quantise_wide(("spline", 5))
-            distances(b1)
+            first_fold(b1)
             inner_piece(a, True)
+            quantise_wide(("spline", 5))
             outer_piece(a)
             inner_product(b)
-            squares(b1)
-            sides(a)
+            refold(b1)
             inner_piece(b, True)
+            collect(1)
+            turn(7)
+            sides(a1)
             join(a)
-            quantise_wide(("spline", 1))
+            sides(b1)
+            squares(b1)
             clip(a)
             join(b)
             sign(a)
+            quantise_wide(("spline", 1))
+            first_fold(a1)
+            split(a)
+            clip(b)
             collect(7)
             turn(3)
-            clip(b)
-            split(a)
-            sides(b)
-            distances(a1)
             quantise_unit(a)
             contract(a)
+            refold(a1)
             sign(b)
-            quantise_wide(("spline", 7))
-            squares(a1)
-            split(b)
             collect(3)
             base_banks = turn_weights(lambda n, s: base_raw[:, n, s * P : (s + 1) * P])
+            squares(a1)
+            split(b)
 
             before = b
             a, b = a1, b1
             outer_piece(b)
             quantise_unit(before)
             inner_product(a)
-            quantise_wide(("spline", 3))
-            contract(before)
+            quantise_wide(("spline", 7))
             inner_piece(a, True)
             outer_piece(a)
             collect_weights(("base",), base_banks)
             inner_product(b)
+            quantise_wide(("spline", 3))
+            contract(before)
             inner_piece(b, True)
-            sides(a)
-            sides(b)
             join(a)
-            quantise_wide(("base",))
-            clip(a)
             grouped["silu"] = work.tile(
                 [P, GROUPS, TOKENS, PACK], BF16, align_bytes=64, tag="w_grouped", name="silu"
             )
             nc.scalar.activation(out=grouped["silu"][:], in_=x_int[:], func=ACT.Silu)
+            quantise_wide(("base",))
+            clip(a)
+            join(b, most)
             sign(a)
-            join(b, halves[0])
+            clip(b, most)
             split(a)
-            clip(b, halves[0])
+            sign(b, most)
             quantise_unit(a)
             contract(a)
-            sign(b, halves[0])
             quantise_wide("silu")
             for q in range(GROUPS):
                 multiply("silu", q * TOKENS, ("base",), q, start=False, stop=False)
-            split(b, halves[0])
-            join(b, halves[1])
-            quantise_unit(b, halves[0])
-            contract(b, (0, 1))
-            clip(b, halves[1])
-            sign(b, halves[1])
-            split(b, halves[1])
-            quantise_unit(b, halves[1])
-            contract(b, (2, 3))
+            split(b, most)
+            join(b, rest)
+            quantise_unit(b, most)
+            contract(b, (0, 1, 2))
+            clip(b, rest)
+            sign(b, rest)
+            split(b, rest)
+            quantise_unit(b, rest)
+            contract(b, (3,))
 
             nc.scalar.activation(out=warm[:], in_=zero[:], func=ACT.Gelu)
             stats = keep.tile([P, TOKEN_TILES, 6], F32)
             mean_var = keep.tile([P, TOKEN_TILES, 2], F32)
             rstd = keep.tile([P, TOKEN_TILES], F32)
             gelu = fold.tile([P, TOKEN_TILES, OUTS], F32, tag="dist", name="gelu")
-            for h in range(2):
-                tiles = (2 * h, 2 * h + 1)
+            for tiles in ((0, 1, 2), (3,)):
                 for m in tiles:
                     nc.scalar.activation(out=gelu[:, m, :], in_=acc[m][:], func=ACT.Gelu)
                 for m in tiles:
                     nc.vector.bn_stats(out=stats[:, m, :], in_=gelu[:, m, :])
                 for m in tiles:
                     nc.vector.bn_aggr(out=mean_var[:, m, :], in_=stats[:, m, :])
-                columns = slice(2 * h, 2 * h + 2)
+                columns = slice(tiles[0], tiles[0] + len(tiles))
                 nc.gpsimd.tensor_scalar(
                     out=rstd[:, columns], in0=mean_var[:, columns, 1], scalar1=EPS, scalar2=0.0, op0=ALU.add, op1=ALU.add
                 )

@@ -19,15 +19,15 @@ FEATURES = 1024
 OUTS = 512
 BASIS = 8
 TOKEN_TILES = TOKENS // P
-QUARTER = FEATURES // 4
-ROWS = P // 4
-BLOCKS = 512 // ROWS
-GROUPS = 2
+OUT_TILES = OUTS // P
+CHUNK = 2 * P
+CHUNKS = FEATURES // CHUNK
 WIDTH = TOKENS * PACK
 WHOLE = slice(0, WIDTH)
+QUARTERS = [slice(m * P * PACK, (m + 1) * P * PACK) for m in range(TOKEN_TILES)]
+MOST, REST = slice(0, 3 * WIDTH // 4), QUARTERS[3]
 EPS = 1e-12
 KNOT_STEP = 0.4
-FIRST_KNOT = -2.2
 KAPPA = math.sqrt(1.0 / 3.0)
 
 FLOPS = 2 * TOKENS * OUTS * (FEATURES + FEATURES * BASIS)
@@ -35,27 +35,28 @@ FLOPS = 2 * TOKENS * OUTS * (FEATURES + FEATURES * BASIS)
 
 def tile_generatorhead_pa_kernel(tc, hidden, base_w1, spline_w1, out):
     nc = tc.nc
-    x_rows = hidden.flatten_outer_dims().rearrange("(n k) (j f) -> (k j) n f", k=ROWS, j=4)
-    base_rows = base_w1.rearrange("(n k) (j f) -> (k j) n f", k=ROWS, j=4)
-    spline_rows = spline_w1.rearrange("(n k) (j f) c -> (k j) n (f c)", k=ROWS, j=4)
+    x_rows = hidden.flatten_outer_dims()
+    base_rows = base_w1.rearrange("(n p) i -> p n i", p=P)
+    spline_rows = spline_w1.rearrange("(n p) i c -> p n (i c)", p=P)
     out_rows = out.flatten_outer_dims()
 
     with ExitStack() as ctx:
         keep = ctx.enter_context(tc.tile_pool(name="keep", bufs=1))
+        wload = ctx.enter_context(tc.tile_pool(name="wload", bufs=3))
         fold = ctx.enter_context(tc.tile_pool(name="fold", bufs=3))
         once = ctx.enter_context(tc.tile_pool(name="once", bufs=1))
         work = ctx.enter_context(tc.tile_pool(name="work", bufs=2))
-        sided = ctx.enter_context(tc.tile_pool(name="sided", bufs=6))
-        mx = ctx.enter_context(tc.tile_pool(name="mx", bufs=7))
-        wmx = ctx.enter_context(tc.tile_pool(name="wmx", bufs=5))
+        sided = ctx.enter_context(tc.tile_pool(name="sided", bufs=4))
+        mx = ctx.enter_context(tc.tile_pool(name="mx", bufs=3))
+        wmx = ctx.enter_context(tc.tile_pool(name="wmx", bufs=4))
         acc_pool = ctx.enter_context(tc.psum_pool(name="acc", bufs=1))
-        turns = ctx.enter_context(tc.psum_pool(name="turns", bufs=4))
+        turns = ctx.enter_context(tc.psum_pool(name="turns", bufs=2))
 
-        x_raw = keep.tile([P, BLOCKS, QUARTER], BF16, tag="raw", name="x_raw")
-        base_raw = keep.tile([P, BLOCKS, QUARTER], BF16, tag="raw", name="base_raw")
-        w_raw = [keep.tile([P, 2, QUARTER * BASIS], BF16, name="w_raw%d" % i) for i in range(BLOCKS // 2)]
-        x_int = keep.tile([P, GROUPS, TOKENS, PACK], BF16)
+        x_raw = keep.tile([P, TOKEN_TILES, FEATURES], BF16)
+        base_raw = keep.tile([P, OUT_TILES, FEATURES], BF16)
         acc = [acc_pool.tile([P, OUTS], F32, name="acc%d" % m) for m in range(TOKEN_TILES)]
+        w_raw = {}
+        near = {}
         dist = {}
         square = {}
         inner = {}
@@ -63,86 +64,147 @@ def tile_generatorhead_pa_kernel(tc, hidden, base_w1, spline_w1, out):
         side = {}
         grouped = {}
         quantised = {}
-        turned = {}
 
-        def turn_bank(source):
-            bank = turns.tile([P, GROUPS, P, 2, 2], BF16, tag="bank", name="bank")
-            for n in range(4):
-                for s in range(2):
-                    nc.tensor.transpose(
-                        bank[:, :, n * ROWS : (n + 1) * ROWS, s, :].rearrange("p q k h -> p k q h"),
-                        source(n, s),
-                        ident[:],
+        def partner(u):
+            return (u[0], 1 - u[1])
+
+        for m in range(TOKEN_TILES):
+            nc.sync.dma_start(out=x_raw[:, m, :], in_=x_rows[m * P : (m + 1) * P, :])
+
+        def load_weights(i):
+            w_raw[i] = wload.tile([P, OUT_TILES, CHUNK * BASIS], BF16, name="w_raw")
+            for half in range(2):
+                tiles = slice(2 * half, 2 * half + 2)
+                nc.sync.dma_start(
+                    out=w_raw[i][:, tiles, :],
+                    in_=spline_rows[:, tiles, i * CHUNK * BASIS : (i + 1) * CHUNK * BASIS],
+                )
+
+        load_weights(0)
+        load_weights(1)
+        nc.sync.dma_start(out=base_raw[:], in_=base_rows)
+        load_weights(2)
+
+        ident = keep.tile([P, P], F32)
+        make_identity(nc, ident[:])
+        scaled = keep.tile([P, P], BF16)
+        nc.vector.tensor_scalar_mul(out=scaled[:], in0=ident[:], scalar1=1.0 / KNOT_STEP)
+        ones = keep.tile([P, P], BF16)
+        nc.vector.memset(ones[:], 1.0)
+        shift = keep.tile([P, P], BF16)
+        nc.vector.memset(shift[:], -1.0 / P)
+        minus_half = keep.tile([P, TOKEN_TILES], F32)
+        nc.gpsimd.memset(minus_half[:], -0.5)
+        zero = keep.tile([P, 1], F32)
+        nc.vector.memset(zero[:], 0.0)
+        warm = keep.tile([P, 1], F32)
+        nc.scalar.activation(out=warm[:], in_=zero[:], func=ACT.Silu)
+
+        zbanks = {}
+
+        def make_z(i, m):
+            bank = turns.tile([P, PACK, P], F32, tag="z", name="z")
+            for u in range(2):
+                first = i * CHUNK + u * P
+                for e in range(2):
+                    nc.tensor.matmul(
+                        bank[:, 2 * u + e, :],
+                        lhsT=x_raw[:, m, first : first + P],
+                        rhs=scaled[:],
+                        start=True,
+                        stop=(e == 0),
                     )
-            return bank
+                nc.tensor.matmul(bank[:, 2 * u + 1, :], lhsT=ones[:], rhs=shift[:], start=False, stop=True)
+            zbanks[i, m] = bank
 
-        def quantise_act(key, src, part):
-            if part.start == 0:
-                codes = mx.tile([P, TOKENS], U32, align_bytes=64, name="act_codes")
-                scales = mx.tile([P, TOKENS], U8, align_bytes=64, name="act_scales")
-                quantised[key] = (codes, scales)
-            codes, scales = quantised[key]
-            for piece in (halves[0], quarters[2]) if part == most else (part,):
-                words = slice(piece.start // PACK, piece.stop // PACK)
-                nc.vector.quantize_mx(out=codes[:, words].bitcast(FP8X4), scales=scales[:, words], in_=src[:, piece])
+        turned = []
 
-        def quantise_wide(key):
-            codes = wmx.tile([P, GROUPS * OUTS], U32, align_bytes=64, name="w_codes")
-            scales = wmx.tile([P, GROUPS * OUTS], U8, align_bytes=64, name="w_scales")
-            nc.vector.quantize_mx(
-                out=codes[:].bitcast(FP8X4), scales=scales[:], in_=grouped[key][:].rearrange("p q o t -> p (q o t)")
-            )
-            quantised[key] = (codes, scales)
+        def turn(source):
+            bank = turns.tile([P, 2, 2, P], F32, tag="w", name="w")
+            for n in range(2):
+                for u in range(2):
+                    nc.tensor.transpose(bank[:, u, n, :], source(n, u), ident[:])
+            turned.append(bank)
 
-        def multiply(act_key, act_first, w_key, q, start, stop, tiles=range(TOKEN_TILES)):
-            act_codes, act_scales = quantised[act_key]
-            w_codes, w_scales = quantised[w_key]
-            outs = slice(q * OUTS, (q + 1) * OUTS)
-            for m in tiles:
-                cols = slice(act_first + m * P, act_first + (m + 1) * P)
-                nc.tensor.matmul_mx(
-                    out=acc[m][:],
-                    lhsT=act_codes[:, cols].bitcast(FP8X4),
-                    lhsT_scale=act_scales[:, cols],
-                    rhs=w_codes[:, outs].bitcast(FP8X4),
-                    rhs_scale=w_scales[:, outs],
-                    start=start,
-                    stop=stop,
-                )
+        def turn_spline(i, s, part, half):
+            w = 2 * (1 - part) + s
+            words = w_raw[i][:].bitcast(F32).rearrange("p n (f w) -> p n f w", w=BASIS // 2)
+            turn(lambda n, u: words[:, 2 * half + n, u * P : (u + 1) * P, w])
 
-        def turn_weights(source):
-            return [turn_bank(lambda n, s: source(4 * b + n, s)) for b in range(OUTS // P)]
+        def turn_raw(raw, g, half):
+            words = raw[:].bitcast(F32)
+            turn(lambda n, u: words[:, 2 * half + n, (2 * g + u) * P : (2 * g + u + 1) * P])
 
-        def collect_weights(key, banks):
-            grouped[key] = work.tile([P, GROUPS, OUTS, PACK], BF16, align_bytes=64, name="w_grouped")
-            for b in range(OUTS // P):
-                rows = grouped[key][:, :, b * P : (b + 1) * P, :].rearrange("p q k t -> p q (k t)")
-                nc.scalar.copy(
-                    out=rows.bitcast(F32), in_=banks[b][:].rearrange("p q k s h -> p q (k s h)").bitcast(F32)
-                )
+        blocks = []
+        for i in range(CHUNKS):
+            for s in range(2):
+                for part in range(2):
+                    for half in range(2):
+                        blocks.append((i, s, part, half))
 
-        def spline_source(c):
-            def block(n, s):
-                rows = w_raw[n // 2][:, n % 2, :].rearrange("p (f c) -> p f c", c=BASIS)
-                return rows[:, s * P : (s + 1) * P, c]
+        others = [(raw, g, half) for raw in (base_raw, x_raw) for g in range(2) for half in range(2)]
 
-            return block
+        def fill(count=1):
+            for j in range(count):
+                if blocks:
+                    turn_spline(*blocks.pop(0))
+                elif others:
+                    turn_raw(*others.pop(0))
 
-        def first_fold(u, part=WHOLE):
-            q, r = u
-            if part.start == 0:
-                dist[u] = fold.tile([P, WIDTH], F32, name="dist")
-            x_flat = x_int[:, q, :, :].rearrange("p k t -> p (k t)")
+        drained = []
+
+        def drain(count=1):
+            for j in range(count):
+                step = len(drained)
+                key = ("w", step // 8, (step // 4) % 2)
+                part, half = (step // 2) % 2, step % 2
+                if part == 0 and half == 0:
+                    grouped[key] = work.tile([P, 2, OUTS, PACK], BF16, align_bytes=64, tag="w_grouped", name="w_grouped")
+                copy_words(grouped[key][:, part, :, :], half, turned.pop(0))
+                drained.append(step)
+                fill()
+
+        def copy_words(target, half, bank):
+            rows = target[:, half * 2 * P : (half + 1) * 2 * P, :].bitcast(F32)
+            nc.scalar.copy(out=rows, in_=bank[:].rearrange("p u n k -> p (n k) u"))
+
+        def drain_base():
+            grouped["base"] = work.tile([P, 2, OUTS, PACK], BF16, align_bytes=64, tag="w_grouped", name="base_grouped")
+            for g in range(2):
+                for half in range(2):
+                    copy_words(grouped["base"][:, g, :, :], half, turned.pop(0))
+                    fill()
+
+        def drain_silu():
+            grouped["silu"] = work.tile([P, 2, TOKENS, PACK], BF16, align_bytes=64, tag="w_grouped", name="silu")
+            for g in range(2):
+                for half in range(2):
+                    bank = turned.pop(0)
+                    pairs = bank[:].rearrange("p u n k -> p u (n k)").bitcast(BF16)
+                    nc.scalar.activation(
+                        out=grouped["silu"][:, g, half * 2 * P : (half + 1) * 2 * P, :].rearrange(
+                            "p k (u e) -> p k u e", u=2
+                        ),
+                        in_=pairs.rearrange("p u (k e) -> p k u e", e=2),
+                        func=ACT.Silu,
+                    )
+                    fill()
+
+        def folds(u, m):
+            i, s = u
+            if m == 0:
+                near[u] = fold.tile([P, WIDTH], F32, name="near")
             nc.scalar.activation(
-                out=dist[u][:, part], in_=x_flat[:, part], func=ACT.Abs, scale=1.0 / KNOT_STEP, bias=1.5 - r
+                out=near[u][:, QUARTERS[m]].rearrange("p (k g) -> p k g", g=PACK),
+                in_=zbanks[i, m][:].rearrange("p g k -> p k g"),
+                func=ACT.Abs,
+                bias=1.5 - 2.0 * s,
             )
 
         def refold(u, part=WHOLE):
-            nc.scalar.activation(out=dist[u][:, part], in_=dist[u][:, part], func=ACT.Abs, bias=-2.0)
-
-        def distances(u):
-            first_fold(u)
-            refold(u)
+            if part.start == 0:
+                dist[u] = fold.tile([P, WIDTH], F32, name="dist")
+            nc.scalar.activation(out=dist[u][:, part], in_=near[u][:, part], func=ACT.Abs, bias=-2.0)
 
         def squares(u, part=WHOLE):
             if part.start == 0:
@@ -150,9 +212,6 @@ def tile_generatorhead_pa_kernel(tc, hidden, base_w1, spline_w1, out):
             nc.scalar.activation(
                 out=square[u][:, part], in_=dist[u][:, part], func=ACT.Square, scale=-KAPPA, bias=2.0 * KAPPA
             )
-
-        def partner(u):
-            return (u[0], (u[1] + 2) % PACK)
 
         def outer_piece(u, part=WHOLE):
             if part.start == 0:
@@ -177,28 +236,24 @@ def tile_generatorhead_pa_kernel(tc, hidden, base_w1, spline_w1, out):
                 op1=ALU.mult,
             )
 
-        def inner_piece(u, on_scalar, part=WHOLE):
-            if part.start == 0:
-                inner[u] = work.tile([P, WIDTH], BF16, name="inner")
-            source = square[partner(u)][:, part]
+        def inner_piece(u, on_scalar=True):
+            inner[u] = work.tile([P, WIDTH], BF16, name="inner")
+            source = square[partner(u)]
             if on_scalar:
-                nc.scalar.activation(
-                    out=inner[u][:, part], in_=source, func=ACT.Identity, scale=-3.0, bias=-4.0 / 3.0
-                )
+                nc.scalar.activation(out=inner[u][:], in_=source[:], func=ACT.Identity, scale=-3.0, bias=-4.0 / 3.0)
             else:
                 nc.vector.tensor_scalar(
-                    out=inner[u][:, part], in0=source, scalar1=-3.0, scalar2=-4.0 / 3.0, op0=ALU.mult, op1=ALU.add
+                    out=inner[u][:], in0=source[:], scalar1=-3.0, scalar2=-4.0 / 3.0, op0=ALU.mult, op1=ALU.add
                 )
 
         def sides(u):
-            q, r = u
             side[u] = sided.tile([P, WIDTH], BF16, name="side")
             nc.vector.tensor_scalar(
                 out=side[u][:],
-                in0=x_int[:, q, :, :].rearrange("p k t -> p (k t)"),
-                scalar1=FIRST_KNOT + KNOT_STEP * (r + PACK),
+                in0=near[partner(u)][:],
+                scalar1=2.0,
                 scalar2=0.5,
-                op0=ALU.is_ge,
+                op0=ALU.is_le if u[1] == 0 else ALU.is_ge,
                 op1=ALU.subtract,
             )
 
@@ -215,239 +270,178 @@ def tile_generatorhead_pa_kernel(tc, hidden, base_w1, spline_w1, out):
             nc.vector.tensor_tensor(out=values, in0=values, in1=side[u][:, part], op=ALU.mult)
 
         def split(u, part=WHOLE):
-            q, r = u
             if part.start == 0:
-                grouped["basis", q, r] = once.tile([P, WIDTH], BF16, align_bytes=64, name="low")
-                grouped["basis", q, r + PACK] = once.tile([P, WIDTH], BF16, align_bytes=64, name="high")
+                grouped[u] = once.tile([P, 2, WIDTH], BF16, align_bytes=64, name="basis")
             nc.vector.tensor_scalar(
-                out=grouped["basis", q, r + PACK][:, part],
-                in0=neg[u][:, part],
-                scalar1=-1.0,
-                scalar2=0.0,
-                op0=ALU.mult,
-                op1=ALU.max,
+                out=grouped[u][:, 0, part], in0=neg[u][:, part], scalar1=-1.0, scalar2=0.0, op0=ALU.mult, op1=ALU.max
             )
-            nc.vector.tensor_scalar_max(out=grouped["basis", q, r][:, part], in0=neg[u][:, part], scalar1=0.0)
+            nc.vector.tensor_scalar_max(out=grouped[u][:, 1, part], in0=neg[u][:, part], scalar1=0.0)
 
-        def quantise_unit(u, part=WHOLE):
-            q, r = u
-            for c in (r + PACK, r):
-                quantise_act(("basis", q, c), grouped["basis", q, c], part)
+        def quantise(pool, key, source, columns):
+            if columns.start == 0 and key not in quantised:
+                codes = pool.tile([P, 2 * OUTS], U32, align_bytes=64, name="codes")
+                scales = pool.tile([P, 2 * OUTS], U8, align_bytes=64, name="scales")
+                quantised[key] = (codes, scales)
+            codes, scales = quantised[key]
+            words = slice(columns.start // PACK, columns.stop // PACK)
+            nc.vector.quantize_mx(
+                out=codes[:, words].bitcast(FP8X4), scales=scales[:, words], in_=source[:, columns]
+            )
 
-        def contract(u, tiles=range(TOKEN_TILES)):
-            q, r = u
-            for c in (r + PACK, r):
-                multiply(
-                    ("basis", q, c),
-                    0,
-                    ("spline", c),
-                    q,
-                    start=(u == units[0] and c == r + PACK),
-                    stop=(u == units[len(units) - 1] and c == r),
-                    tiles=tiles,
-                )
+        def quantise_unit(u):
+            quantise(mx, u, grouped[u][:].rearrange("p h k -> p (h k)"), slice(0, 2 * WIDTH))
 
-        def turn(c):
-            turned[c] = turn_weights(spline_source(c))
+        def quantise_pieces(u, pieces):
+            for piece in pieces:
+                for h in range(2):
+                    quantise(
+                        mx,
+                        u,
+                        grouped[u][:].rearrange("p h k -> p (h k)"),
+                        slice(h * WIDTH + piece.start, h * WIDTH + piece.stop),
+                    )
 
-        def collect(c):
-            collect_weights(("spline", c), turned[c])
+        def quantise_weights(key):
+            quantise(wmx, key, grouped[key][:].rearrange("p h o t -> p (h o t)"), slice(0, 2 * WIDTH))
 
-        for b in range(TOKEN_TILES):
-            nc.sync.dma_start(out=x_raw[:, 4 * b : 4 * b + 4, :], in_=x_rows[:, 4 * b : 4 * b + 4, :])
-        for i in range(BLOCKS // 2):
-            nc.sync.dma_start(out=w_raw[i][:], in_=spline_rows[:, 2 * i : 2 * i + 2, :])
+        opened = []
 
-        ident = keep.tile([P, P], BF16)
-        make_identity(nc, ident[:])
-        zero = keep.tile([P, 1], F32)
-        nc.vector.memset(zero[:], 0.0)
-        minus_half = keep.tile([P, TOKEN_TILES], F32)
-        nc.gpsimd.memset(minus_half[:], -0.5)
-        warm = keep.tile([P, 1], F32)
-        nc.scalar.activation(out=warm[:], in_=zero[:], func=ACT.Silu)
+        def contract(act_key, w_key, tiles=range(TOKEN_TILES), last=False):
+            act_codes, act_scales = quantised[act_key]
+            w_codes, w_scales = quantised[w_key]
+            for m in tiles:
+                for h in range(2):
+                    cols = slice(h * TOKENS + m * P, h * TOKENS + (m + 1) * P)
+                    outs = slice(h * OUTS, (h + 1) * OUTS)
+                    nc.tensor.matmul_mx(
+                        out=acc[m][:],
+                        lhsT=act_codes[:, cols].bitcast(FP8X4),
+                        lhsT_scale=act_scales[:, cols],
+                        rhs=w_codes[:, outs].bitcast(FP8X4),
+                        rhs_scale=w_scales[:, outs],
+                        start=m not in opened,
+                        stop=last and h == 1,
+                    )
+                    opened.append(m)
 
-        pairs = [((q, r), (q, r + 2)) for r in range(2) for q in range(GROUPS)]
-        units = [u for pair in pairs for u in pair]
-        halves = [slice(0, WIDTH // 2), slice(WIDTH // 2, WIDTH)]
-        most, rest = slice(0, 3 * WIDTH // 4), slice(3 * WIDTH // 4, WIDTH)
-        quarters = [slice(b * P * PACK, (b + 1) * P * PACK) for b in range(TOKEN_TILES)]
-        steps = [slice(0, WIDTH // 4), slice(WIDTH // 4, WIDTH // 2), halves[1]]
-
-        def products(a, b, part):
-            outer_piece(b, part)
-            inner_product(a, part)
-            outer_piece(a, part)
-            inner_product(b, part)
+        def product(u, tiles=range(TOKEN_TILES), last=False):
+            contract(u, ("w", u[0], u[1]), tiles, last)
 
         with tc.manual_schedule():
-            for b in range(TOKEN_TILES):
-                nc.vector.tensor_copy(
-                    out=x_int[:, :, b * P : (b + 1) * P, :],
-                    in_=turn_bank(lambda n, s: x_raw[:, 4 * b + n, s * P : (s + 1) * P])[:].rearrange(
-                        "p q k s h -> p q k (s h)"
-                    ),
-                )
-            nc.sync.dma_start(out=base_raw[:], in_=base_rows)
-            a, b = pairs[0]
-            a1, b1 = pairs[1]
-            for part in steps:
-                first_fold(b, part)
-                first_fold(a, part)
+            a, b = (0, 0), (0, 1)
+            make_z(0, 0)
+            make_z(0, 1)
+            fill(2)
+            for m in range(TOKEN_TILES):
+                part = QUARTERS[m]
+                folds(b, m)
+                folds(a, m)
+                if m + 2 < TOKEN_TILES:
+                    make_z(0, m + 2)
                 refold(b, part)
                 refold(a, part)
                 squares(b, part)
                 squares(a, part)
-                products(a, b, part)
-                if part == steps[0]:
+                if m == 3:
                     sides(a)
                     sides(b)
-                    sides(a1)
-                if part == steps[1]:
-                    sides(b1)
-                    sides(pairs[2][0])
-                    inner_piece(a, False, halves[0])
-                    join(a, halves[0])
+                outer_piece(b, part)
+                inner_product(a, part)
+                outer_piece(a, part)
+                inner_product(b, part)
+            make_z(1, 0)
+            make_z(1, 1)
 
-            turn(4)
-            distances(b1)
-            squares(b1)
-            inner_piece(b, False, halves[0])
-            inner_piece(a, False, halves[1])
-            inner_piece(b, False, halves[1])
-            join(a, halves[1])
-            join(b)
-            clip(a)
-            clip(b)
-            sign(a)
-            collect(4)
-            turn(0)
-            sign(b)
-            split(a)
-            quantise_unit(a)
-            distances(a1)
-            squares(a1)
-            collect(0)
-            turn(6)
-            quantise_wide(("spline", 4))
-            split(b)
+            before = None
+            for i in range(CHUNKS - 1):
+                a, b = (i, 0), (i, 1)
+                a1, b1 = (i + 1, 0), (i + 1, 1)
+                if before:
+                    outer_piece(b)
+                    quantise_unit(before)
+                folds(b1, 0)
+                folds(a1, 0)
+                make_z(i + 1, 2)
+                if before:
+                    inner_product(a)
+                folds(b1, 1)
+                folds(a1, 1)
+                make_z(i + 1, 3)
+                drain(4)
+                if before:
+                    product(before)
+                    outer_piece(a)
+                    inner_product(b)
+                inner_piece(a, on_scalar=i > 0)
+                folds(b1, 2)
+                folds(a1, 2)
+                folds(b1, 3)
+                folds(a1, 3)
+                inner_piece(b, on_scalar=i > 0)
+                join(a)
+                quantise_weights(("w", i, 0))
+                clip(a)
+                join(b)
+                refold(b1)
+                sign(a)
+                clip(b)
+                drain(2)
+                split(a)
+                sides(b1)
+                quantise_unit(a)
+                refold(a1)
+                sign(b)
+                sides(a1)
+                drain(2)
+                if i + 2 < CHUNKS:
+                    make_z(i + 2, 0)
+                    make_z(i + 2, 1)
+                product(a)
+                quantise_weights(("w", i, 1))
+                squares(b1)
+                squares(a1)
+                split(b)
+                if i + 3 < CHUNKS:
+                    load_weights(i + 3)
+                before = b
 
-            before = b
-            a, b = a1, b1
-            a1, b1 = pairs[2]
+            a, b = (CHUNKS - 1, 0), (CHUNKS - 1, 1)
+            drain(4)
             outer_piece(b)
             quantise_unit(before)
             inner_product(a)
-            first_fold(b1)
-            inner_piece(a, True)
-            quantise_wide(("spline", 0))
-            contract(units[0])
+            drain(2)
+            inner_piece(a)
             outer_piece(a)
+            quantise_weights(("w", CHUNKS - 1, 0))
             inner_product(b)
-            refold(b1)
-            inner_piece(b, True)
-            collect(6)
-            turn(2)
+            drain(2)
+            product(before)
+            inner_piece(b)
             join(a)
-            sides(b1)
-            squares(b1)
+            drain_base()
+            quantise_weights(("w", CHUNKS - 1, 1))
             clip(a)
-            join(b)
+            drain_silu()
+            join(b, MOST)
             sign(a)
-            quantise_wide(("spline", 6))
-            collect(2)
-            turn(5)
+            quantise_weights("base")
+            clip(b, MOST)
             split(a)
-            clip(b)
-            first_fold(a1)
+            sign(b, MOST)
             quantise_unit(a)
-            contract(a)
-            collect(5)
-            turn(1)
-            sign(b)
-            quantise_wide(("spline", 2))
-            contract(before)
-            refold(a1)
-            squares(a1)
-            split(b)
-
-            before = b
-            a, b = a1, b1
-            a1, b1 = pairs[3]
-            outer_piece(b)
-            quantise_unit(before)
-            contract(before)
-            inner_product(a)
-            first_fold(b1)
-            inner_piece(a, True)
-            quantise_wide(("spline", 5))
-            outer_piece(a)
-            inner_product(b)
-            refold(b1)
-            inner_piece(b, True)
-            collect(1)
-            turn(7)
-            sides(a1)
-            join(a)
-            sides(b1)
-            squares(b1)
-            clip(a)
-            join(b)
-            sign(a)
-            quantise_wide(("spline", 1))
-            first_fold(a1)
-            split(a)
-            clip(b)
-            collect(7)
-            turn(3)
-            quantise_unit(a)
-            contract(a)
-            refold(a1)
-            sign(b)
-            collect(3)
-            base_banks = turn_weights(lambda n, s: base_raw[:, n, s * P : (s + 1) * P])
-            squares(a1)
-            split(b)
-
-            before = b
-            a, b = a1, b1
-            outer_piece(b)
-            quantise_unit(before)
-            inner_product(a)
-            quantise_wide(("spline", 7))
-            inner_piece(a, True)
-            outer_piece(a)
-            collect_weights(("base",), base_banks)
-            inner_product(b)
-            quantise_wide(("spline", 3))
-            contract(before)
-            inner_piece(b, True)
-            join(a)
-            grouped["silu"] = work.tile(
-                [P, GROUPS, TOKENS, PACK], BF16, align_bytes=64, tag="w_grouped", name="silu"
-            )
-            nc.scalar.activation(out=grouped["silu"][:], in_=x_int[:], func=ACT.Silu)
-            quantise_wide(("base",))
-            clip(a)
-            join(b, most)
-            sign(a)
-            clip(b, most)
-            split(a)
-            sign(b, most)
-            quantise_unit(a)
-            contract(a)
-            quantise_wide("silu")
-            for q in range(GROUPS):
-                multiply("silu", q * TOKENS, ("base",), q, start=False, stop=False)
-            split(b, most)
-            join(b, rest)
-            quantise_unit(b, most)
-            contract(b, (0, 1, 2))
-            clip(b, rest)
-            sign(b, rest)
-            split(b, rest)
-            quantise_unit(b, rest)
-            contract(b, (3,))
+            product(a)
+            split(b, MOST)
+            join(b, REST)
+            quantise(mx, "silu", grouped["silu"][:].rearrange("p g k t -> p (g k t)"), slice(0, 2 * WIDTH))
+            contract("silu", "base")
+            clip(b, REST)
+            quantise_pieces(b, (slice(0, WIDTH // 2), QUARTERS[2]))
+            product(b, (0, 1, 2), last=True)
+            sign(b, REST)
+            split(b, REST)
+            quantise_pieces(b, (QUARTERS[3],))
+            product(b, (3,), last=True)
 
             nc.scalar.activation(out=warm[:], in_=zero[:], func=ACT.Gelu)
             stats = keep.tile([P, TOKEN_TILES, 6], F32)
@@ -468,13 +462,13 @@ def tile_generatorhead_pa_kernel(tc, hidden, base_w1, spline_w1, out):
                 nc.gpsimd.tensor_tensor(
                     out=rstd[:, columns], in0=rstd[:, columns], in1=minus_half[:, columns], op=ALU.pow
                 )
-                for m in tiles:
-                    nc.vector.tensor_scalar(
-                        out=gelu[:, m, :],
-                        in0=gelu[:, m, :],
-                        scalar1=mean_var[:, m, 0:1],
-                        scalar2=rstd[:, m : m + 1],
-                        op0=ALU.subtract,
-                        op1=ALU.mult,
-                    )
-                    nc.sync.dma_start(out=out_rows[m * P : (m + 1) * P, :], in_=gelu[:, m, :])
+            for m in range(TOKEN_TILES):
+                nc.vector.tensor_scalar(
+                    out=gelu[:, m, :],
+                    in0=gelu[:, m, :],
+                    scalar1=mean_var[:, m, 0:1],
+                    scalar2=rstd[:, m : m + 1],
+                    op0=ALU.subtract,
+                    op1=ALU.mult,
+                )
+                nc.sync.dma_start(out=out_rows[m * P : (m + 1) * P, :], in_=gelu[:, m, :])

@@ -35,7 +35,7 @@ FLOPS = 2 * TOKENS * OUTS * (FEATURES + FEATURES * BASIS)
 
 def tile_generatorhead_pa_kernel(tc, hidden, base_w1, spline_w1, out):
     nc = tc.nc
-    x_rows = hidden.flatten_outer_dims()
+    x_rows = hidden.flatten_outer_dims().rearrange("(m p) i -> p m i", p=P)
     base_rows = base_w1.rearrange("(n p) i -> p n i", p=P)
     spline_rows = spline_w1.rearrange("(n p) i c -> p n (i c)", p=P)
     out_rows = out.flatten_outer_dims()
@@ -62,14 +62,19 @@ def tile_generatorhead_pa_kernel(tc, hidden, base_w1, spline_w1, out):
         inner = {}
         neg = {}
         side = {}
+        by_scalar = []
         grouped = {}
         quantised = {}
 
         def partner(u):
             return (u[0], 1 - u[1])
 
-        for m in range(TOKEN_TILES):
-            nc.sync.dma_start(out=x_raw[:, m, :], in_=x_rows[m * P : (m + 1) * P, :])
+        for tiles, columns in (
+            (slice(0, 1), slice(0, CHUNK)),
+            (slice(1, TOKEN_TILES), slice(0, CHUNK)),
+            (slice(0, TOKEN_TILES), slice(CHUNK, FEATURES)),
+        ):
+            nc.sync.dma_start(out=x_raw[:, tiles, columns], in_=x_rows[:, tiles, columns])
 
         def load_weights(i):
             w_raw[i] = wload.tile([P, OUT_TILES, CHUNK * BASIS], BF16, name="w_raw")
@@ -190,13 +195,14 @@ def tile_generatorhead_pa_kernel(tc, hidden, base_w1, spline_w1, out):
                     )
                     fill()
 
-        def folds(u, m):
+        def folds(u, m, tokens=slice(0, P)):
             i, s = u
-            if m == 0:
+            if m == 0 and tokens.start == 0:
                 near[u] = fold.tile([P, WIDTH], F32, name="near")
+            columns = slice((m * P + tokens.start) * PACK, (m * P + tokens.stop) * PACK)
             nc.scalar.activation(
-                out=near[u][:, QUARTERS[m]].rearrange("p (k g) -> p k g", g=PACK),
-                in_=zbanks[i, m][:].rearrange("p g k -> p k g"),
+                out=near[u][:, columns].rearrange("p (k g) -> p k g", g=PACK),
+                in_=zbanks[i, m][:, :, tokens].rearrange("p g k -> p k g"),
                 func=ACT.Abs,
                 bias=1.5 - 2.0 * s,
             )
@@ -236,26 +242,45 @@ def tile_generatorhead_pa_kernel(tc, hidden, base_w1, spline_w1, out):
                 op1=ALU.mult,
             )
 
-        def inner_piece(u, on_scalar=True):
-            inner[u] = work.tile([P, WIDTH], BF16, name="inner")
-            source = square[partner(u)]
+        def inner_piece(u, on_scalar=True, part=WHOLE):
+            if part.start == 0:
+                inner[u] = work.tile([P, WIDTH], BF16, name="inner")
+            source = square[partner(u)][:, part]
             if on_scalar:
-                nc.scalar.activation(out=inner[u][:], in_=source[:], func=ACT.Identity, scale=-3.0, bias=-4.0 / 3.0)
+                nc.scalar.activation(
+                    out=inner[u][:, part], in_=source, func=ACT.Identity, scale=-3.0, bias=-4.0 / 3.0
+                )
             else:
                 nc.vector.tensor_scalar(
-                    out=inner[u][:], in0=source[:], scalar1=-3.0, scalar2=-4.0 / 3.0, op0=ALU.mult, op1=ALU.add
+                    out=inner[u][:, part], in0=source, scalar1=-3.0, scalar2=-4.0 / 3.0, op0=ALU.mult, op1=ALU.add
                 )
 
-        def sides(u):
-            side[u] = sided.tile([P, WIDTH], BF16, name="side")
+        def sides(u, part=WHOLE):
+            if part.start == 0:
+                side[u] = sided.tile([P, WIDTH], BF16, name="side")
             nc.vector.tensor_scalar(
-                out=side[u][:],
-                in0=near[partner(u)][:],
+                out=side[u][:, part],
+                in0=near[partner(u)][:, part],
                 scalar1=2.0,
                 scalar2=0.5,
                 op0=ALU.is_le if u[1] == 0 else ALU.is_ge,
                 op1=ALU.subtract,
             )
+
+        def sides_on_scalar(u):
+            side[u] = sided.tile([P, WIDTH], BF16, name="side")
+            by_scalar.append(u)
+            turned_round = u[1] == 0
+            nc.scalar.activation(
+                out=side[u][:],
+                in_=near[partner(u)][:],
+                func=ACT.Sign,
+                scale=-1.0 if turned_round else 1.0,
+                bias=2.0 if turned_round else -2.0,
+            )
+
+        def size(u):
+            return 0.5 if u in by_scalar else 1.0
 
         def join(u, part=WHOLE):
             values = neg[u][:, part]
@@ -273,9 +298,11 @@ def tile_generatorhead_pa_kernel(tc, hidden, base_w1, spline_w1, out):
             if part.start == 0:
                 grouped[u] = once.tile([P, 2, WIDTH], BF16, align_bytes=64, name="basis")
             nc.vector.tensor_scalar(
-                out=grouped[u][:, 0, part], in0=neg[u][:, part], scalar1=-1.0, scalar2=0.0, op0=ALU.mult, op1=ALU.max
+                out=grouped[u][:, 0, part], in0=neg[u][:, part], scalar1=-size(u), scalar2=0.0, op0=ALU.mult, op1=ALU.max
             )
-            nc.vector.tensor_scalar_max(out=grouped[u][:, 1, part], in0=neg[u][:, part], scalar1=0.0)
+            nc.vector.tensor_scalar(
+                out=grouped[u][:, 1, part], in0=neg[u][:, part], scalar1=size(u), scalar2=0.0, op0=ALU.mult, op1=ALU.max
+            )
 
         def quantise(pool, key, source, columns):
             if columns.start == 0 and key not in quantised:
@@ -332,25 +359,35 @@ def tile_generatorhead_pa_kernel(tc, hidden, base_w1, spline_w1, out):
             make_z(0, 0)
             make_z(0, 1)
             fill(2)
-            for m in range(TOKEN_TILES):
-                part = QUARTERS[m]
-                folds(b, m)
-                folds(a, m)
-                if m + 2 < TOKEN_TILES:
+            halves = (slice(0, P // 2), slice(P // 2, P))
+            steps = [(0, halves[0]), (0, halves[1])] + [(m, slice(0, P)) for m in range(1, TOKEN_TILES)]
+            for step in range(len(steps)):
+                m, tokens = steps[step]
+                part = slice((m * P + tokens.start) * PACK, (m * P + tokens.stop) * PACK)
+                folds(b, m, tokens)
+                folds(a, m, tokens)
+                if tokens.stop == P and m + 2 < TOKEN_TILES:
                     make_z(0, m + 2)
                 refold(b, part)
                 refold(a, part)
                 squares(b, part)
                 squares(a, part)
+                if m > 0:
+                    sides(a, QUARTERS[m - 1])
+                    inner_piece(a, False, QUARTERS[m - 1])
+                    sides(b, QUARTERS[m - 1])
+                    inner_piece(b, False, QUARTERS[m - 1])
                 if m == 3:
-                    sides(a)
-                    sides(b)
+                    sides(a, QUARTERS[3])
+                    sides(b, QUARTERS[3])
                 outer_piece(b, part)
                 inner_product(a, part)
                 outer_piece(a, part)
                 inner_product(b, part)
             make_z(1, 0)
             make_z(1, 1)
+            inner_piece(a, False, QUARTERS[3])
+            inner_piece(b, False, QUARTERS[3])
 
             before = None
             for i in range(CHUNKS - 1):
@@ -364,50 +401,70 @@ def tile_generatorhead_pa_kernel(tc, hidden, base_w1, spline_w1, out):
                 make_z(i + 1, 2)
                 if before:
                     inner_product(a)
+                drain(2)
                 folds(b1, 1)
                 folds(a1, 1)
                 make_z(i + 1, 3)
-                drain(4)
-                if before:
-                    product(before)
-                    outer_piece(a)
-                    inner_product(b)
-                inner_piece(a, on_scalar=i > 0)
                 folds(b1, 2)
                 folds(a1, 2)
+                if before:
+                    inner_piece(a)
+                    outer_piece(a)
+                    inner_product(b)
+                drain(2)
+                if before:
+                    product(before)
                 folds(b1, 3)
                 folds(a1, 3)
-                inner_piece(b, on_scalar=i > 0)
+                if before:
+                    inner_piece(b)
                 join(a)
-                quantise_weights(("w", i, 0))
+                if i == 0:
+                    join(b)
+                else:
+                    quantise_weights(("w", i, 0))
                 clip(a)
-                join(b)
+                if i > 0:
+                    join(b)
                 refold(b1)
-                sign(a)
-                clip(b)
                 drain(2)
+                if i == 0:
+                    clip(b)
+                sign(a)
+                if i == 0:
+                    sign(b)
+                else:
+                    clip(b)
                 split(a)
-                sides(b1)
+                if i < 2:
+                    sides(b1)
+                if i == 0:
+                    quantise_weights(("w", i, 0))
                 quantise_unit(a)
                 refold(a1)
-                sign(b)
-                sides(a1)
+                if i > 0:
+                    sign(b)
+                if i == 0:
+                    sides(a1)
+                if i == 1:
+                    sides_on_scalar(a1)
                 drain(2)
                 if i + 2 < CHUNKS:
                     make_z(i + 2, 0)
                     make_z(i + 2, 1)
                 product(a)
-                quantise_weights(("w", i, 1))
                 squares(b1)
                 squares(a1)
                 split(b)
+                quantise_weights(("w", i, 1))
                 if i + 3 < CHUNKS:
                     load_weights(i + 3)
                 before = b
 
             a, b = (CHUNKS - 1, 0), (CHUNKS - 1, 1)
-            drain(4)
+            drain(2)
             outer_piece(b)
+            sides_on_scalar(a)
             quantise_unit(before)
             inner_product(a)
             drain(2)
@@ -417,27 +474,29 @@ def tile_generatorhead_pa_kernel(tc, hidden, base_w1, spline_w1, out):
             inner_product(b)
             drain(2)
             product(before)
+            sides(b)
             inner_piece(b)
             join(a)
+            drain(2)
             drain_base()
-            quantise_weights(("w", CHUNKS - 1, 1))
             clip(a)
-            drain_silu()
             join(b, MOST)
             sign(a)
-            quantise_weights("base")
             clip(b, MOST)
+            drain_silu()
             split(a)
-            sign(b, MOST)
+            quantise_weights(("w", CHUNKS - 1, 1))
             quantise_unit(a)
+            quantise_weights("base")
             product(a)
-            split(b, MOST)
-            join(b, REST)
+            sign(b, MOST)
             quantise(mx, "silu", grouped["silu"][:].rearrange("p g k t -> p (g k t)"), slice(0, 2 * WIDTH))
             contract("silu", "base")
-            clip(b, REST)
+            split(b, MOST)
+            join(b, REST)
             quantise_pieces(b, (slice(0, WIDTH // 2), QUARTERS[2]))
             product(b, (0, 1, 2), last=True)
+            clip(b, REST)
             sign(b, REST)
             split(b, REST)
             quantise_pieces(b, (QUARTERS[3],))
@@ -448,21 +507,25 @@ def tile_generatorhead_pa_kernel(tc, hidden, base_w1, spline_w1, out):
             mean_var = keep.tile([P, TOKEN_TILES, 2], F32)
             rstd = keep.tile([P, TOKEN_TILES], F32)
             gelu = fold.tile([P, TOKEN_TILES, OUTS], F32, tag="dist", name="gelu")
-            for tiles in ((0, 1, 2), (3,)):
-                for m in tiles:
-                    nc.scalar.activation(out=gelu[:, m, :], in_=acc[m][:], func=ACT.Gelu)
-                for m in tiles:
-                    nc.vector.bn_stats(out=stats[:, m, :], in_=gelu[:, m, :])
-                for m in tiles:
-                    nc.vector.bn_aggr(out=mean_var[:, m, :], in_=stats[:, m, :])
-                columns = slice(tiles[0], tiles[0] + len(tiles))
+
+            def statistics(m):
+                nc.vector.bn_stats(out=stats[:, m, :], in_=gelu[:, m, :])
+
+            def deviation(m):
+                nc.vector.bn_aggr(out=mean_var[:, m, :], in_=stats[:, m, :])
                 nc.gpsimd.tensor_scalar(
-                    out=rstd[:, columns], in0=mean_var[:, columns, 1], scalar1=EPS, scalar2=0.0, op0=ALU.add, op1=ALU.add
+                    out=rstd[:, m : m + 1],
+                    in0=mean_var[:, m, 1:2],
+                    scalar1=EPS,
+                    scalar2=0.0,
+                    op0=ALU.add,
+                    op1=ALU.add,
                 )
                 nc.gpsimd.tensor_tensor(
-                    out=rstd[:, columns], in0=rstd[:, columns], in1=minus_half[:, columns], op=ALU.pow
+                    out=rstd[:, m : m + 1], in0=rstd[:, m : m + 1], in1=minus_half[:, m : m + 1], op=ALU.pow
                 )
-            for m in range(TOKEN_TILES):
+
+            def normalise(m):
                 nc.vector.tensor_scalar(
                     out=gelu[:, m, :],
                     in0=gelu[:, m, :],
@@ -472,3 +535,18 @@ def tile_generatorhead_pa_kernel(tc, hidden, base_w1, spline_w1, out):
                     op1=ALU.mult,
                 )
                 nc.sync.dma_start(out=out_rows[m * P : (m + 1) * P, :], in_=gelu[:, m, :])
+
+            for m in range(TOKEN_TILES):
+                nc.scalar.activation(out=gelu[:, m, :], in_=acc[m][:], func=ACT.Gelu)
+            statistics(0)
+            statistics(1)
+            deviation(0)
+            statistics(2)
+            deviation(1)
+            normalise(0)
+            deviation(2)
+            statistics(3)
+            normalise(1)
+            deviation(3)
+            normalise(2)
+            normalise(3)

@@ -389,164 +389,164 @@ def tile_generatorhead_pa_kernel(tc, hidden, base_w1, spline_w1, out):
             inner_piece(a, False, QUARTERS[3])
             inner_piece(b, False, QUARTERS[3])
 
-            before = None
-            for i in range(CHUNKS - 1):
-                a, b = (i, 0), (i, 1)
-                a1, b1 = (i + 1, 0), (i + 1, 1)
-                if before:
-                    outer_piece(b)
-                    quantise_unit(before)
-                folds(b1, 0)
-                folds(a1, 0)
-                make_z(i + 1, 2)
-                if before:
-                    inner_product(a)
-                drain(2)
-                folds(b1, 1)
-                folds(a1, 1)
-                make_z(i + 1, 3)
-                folds(b1, 2)
-                folds(a1, 2)
-                if before:
-                    inner_piece(a)
-                    outer_piece(a)
-                    inner_product(b)
-                drain(2)
-                if before:
-                    product(before)
-                folds(b1, 3)
-                folds(a1, 3)
-                if before:
-                    inner_piece(b)
-                join(a)
-                if i == 0:
-                    join(b)
-                else:
-                    quantise_weights(("w", i, 0))
-                clip(a)
-                if i > 0:
-                    join(b)
-                refold(b1)
-                drain(2)
-                if i == 0:
-                    clip(b)
-                sign(a)
-                if i == 0:
-                    sign(b)
-                else:
-                    clip(b)
-                split(a)
-                if i < 2:
-                    sides(b1)
-                if i == 0:
-                    quantise_weights(("w", i, 0))
-                quantise_unit(a)
-                refold(a1)
-                if i > 0:
-                    sign(b)
-                if i == 0:
-                    sides(a1)
-                if i == 1:
-                    sides_on_scalar(a1)
-                drain(2)
-                if i + 2 < CHUNKS:
-                    make_z(i + 2, 0)
-                    make_z(i + 2, 1)
-                product(a)
-                squares(b1)
-                squares(a1)
-                split(b)
-                quantise_weights(("w", i, 1))
-                if i + 3 < CHUNKS:
-                    load_weights(i + 3)
-                before = b
-
-            a, b = (CHUNKS - 1, 0), (CHUNKS - 1, 1)
+        before = None
+        for i in range(CHUNKS - 1):
+            a, b = (i, 0), (i, 1)
+            a1, b1 = (i + 1, 0), (i + 1, 1)
+            if before:
+                outer_piece(b)
+                quantise_unit(before)
+            folds(b1, 0)
+            folds(a1, 0)
+            make_z(i + 1, 2)
+            if before:
+                inner_product(a)
             drain(2)
-            outer_piece(b)
-            sides_on_scalar(a)
-            quantise_unit(before)
-            inner_product(a)
+            folds(b1, 1)
+            folds(a1, 1)
+            make_z(i + 1, 3)
+            folds(b1, 2)
+            folds(a1, 2)
+            if before:
+                inner_piece(a)
+                outer_piece(a)
+                inner_product(b)
             drain(2)
-            inner_piece(a)
-            outer_piece(a)
-            quantise_weights(("w", CHUNKS - 1, 0))
-            inner_product(b)
-            drain(2)
-            product(before)
-            sides(b)
-            inner_piece(b)
+            if before:
+                product(before)
+            folds(b1, 3)
+            folds(a1, 3)
+            if before:
+                inner_piece(b)
             join(a)
-            drain(2)
-            drain_base()
+            if i == 0:
+                join(b)
+            else:
+                quantise_weights(("w", i, 0))
             clip(a)
-            join(b, MOST)
+            if i > 0:
+                join(b)
+            refold(b1)
+            drain(2)
+            if i == 0:
+                clip(b)
             sign(a)
-            clip(b, MOST)
-            drain_silu()
+            if i == 0:
+                sign(b)
+            else:
+                clip(b)
             split(a)
-            quantise_weights(("w", CHUNKS - 1, 1))
+            if i < 2:
+                sides(b1)
+            if i == 0:
+                quantise_weights(("w", i, 0))
             quantise_unit(a)
-            quantise_weights("base")
+            refold(a1)
+            if i > 0:
+                sign(b)
+            if i == 0:
+                sides(a1)
+            if i == 1:
+                sides_on_scalar(a1)
+            drain(2)
+            if i + 2 < CHUNKS:
+                make_z(i + 2, 0)
+                make_z(i + 2, 1)
             product(a)
-            sign(b, MOST)
-            quantise(mx, "silu", grouped["silu"][:].rearrange("p g k t -> p (g k t)"), slice(0, 2 * WIDTH))
-            contract("silu", "base")
-            split(b, MOST)
-            join(b, REST)
-            quantise_pieces(b, (slice(0, WIDTH // 2), QUARTERS[2]))
-            product(b, (0, 1, 2), last=True)
-            clip(b, REST)
-            sign(b, REST)
-            split(b, REST)
-            quantise_pieces(b, (QUARTERS[3],))
-            product(b, (3,), last=True)
+            squares(b1)
+            squares(a1)
+            split(b)
+            quantise_weights(("w", i, 1))
+            if i + 3 < CHUNKS:
+                load_weights(i + 3)
+            before = b
 
-            nc.scalar.activation(out=warm[:], in_=zero[:], func=ACT.Gelu)
-            stats = keep.tile([P, TOKEN_TILES, 6], F32)
-            mean_var = keep.tile([P, TOKEN_TILES, 2], F32)
-            rstd = keep.tile([P, TOKEN_TILES], F32)
-            gelu = fold.tile([P, TOKEN_TILES, OUTS], F32, tag="dist", name="gelu")
+        a, b = (CHUNKS - 1, 0), (CHUNKS - 1, 1)
+        drain(2)
+        outer_piece(b)
+        sides_on_scalar(a)
+        quantise_unit(before)
+        inner_product(a)
+        drain(2)
+        inner_piece(a)
+        outer_piece(a)
+        quantise_weights(("w", CHUNKS - 1, 0))
+        inner_product(b)
+        drain(2)
+        product(before)
+        sides(b)
+        inner_piece(b)
+        join(a)
+        drain(2)
+        drain_base()
+        clip(a)
+        join(b, MOST)
+        sign(a)
+        clip(b, MOST)
+        drain_silu()
+        split(a)
+        quantise_weights(("w", CHUNKS - 1, 1))
+        quantise_unit(a)
+        quantise_weights("base")
+        product(a)
+        sign(b, MOST)
+        quantise(mx, "silu", grouped["silu"][:].rearrange("p g k t -> p (g k t)"), slice(0, 2 * WIDTH))
+        contract("silu", "base")
+        split(b, MOST)
+        join(b, REST)
+        quantise_pieces(b, (slice(0, WIDTH // 2), QUARTERS[2]))
+        product(b, (0, 1, 2), last=True)
+        clip(b, REST)
+        sign(b, REST)
+        split(b, REST)
+        quantise_pieces(b, (QUARTERS[3],))
+        product(b, (3,), last=True)
 
-            def statistics(m):
-                nc.vector.bn_stats(out=stats[:, m, :], in_=gelu[:, m, :])
+        nc.scalar.activation(out=warm[:], in_=grouped["silu"][:, 1, TOKENS - 1, 0:1], func=ACT.Gelu)
+        stats = keep.tile([P, TOKEN_TILES, 6], F32)
+        mean_var = keep.tile([P, TOKEN_TILES, 2], F32)
+        rstd = keep.tile([P, TOKEN_TILES], F32)
+        gelu = fold.tile([P, TOKEN_TILES, OUTS], F32, tag="dist", name="gelu")
 
-            def deviation(m):
-                nc.vector.bn_aggr(out=mean_var[:, m, :], in_=stats[:, m, :])
-                nc.gpsimd.tensor_scalar(
-                    out=rstd[:, m : m + 1],
-                    in0=mean_var[:, m, 1:2],
-                    scalar1=EPS,
-                    scalar2=0.0,
-                    op0=ALU.add,
-                    op1=ALU.add,
-                )
-                nc.gpsimd.tensor_tensor(
-                    out=rstd[:, m : m + 1], in0=rstd[:, m : m + 1], in1=minus_half[:, m : m + 1], op=ALU.pow
-                )
+        def statistics(m):
+            nc.vector.bn_stats(out=stats[:, m, :], in_=gelu[:, m, :])
 
-            def normalise(m):
-                nc.vector.tensor_scalar(
-                    out=gelu[:, m, :],
-                    in0=gelu[:, m, :],
-                    scalar1=mean_var[:, m, 0:1],
-                    scalar2=rstd[:, m : m + 1],
-                    op0=ALU.subtract,
-                    op1=ALU.mult,
-                )
-                nc.sync.dma_start(out=out_rows[m * P : (m + 1) * P, :], in_=gelu[:, m, :])
+        def deviation(m):
+            nc.vector.bn_aggr(out=mean_var[:, m, :], in_=stats[:, m, :])
+            nc.gpsimd.tensor_scalar(
+                out=rstd[:, m : m + 1],
+                in0=mean_var[:, m, 1:2],
+                scalar1=EPS,
+                scalar2=0.0,
+                op0=ALU.add,
+                op1=ALU.add,
+            )
+            nc.gpsimd.tensor_tensor(
+                out=rstd[:, m : m + 1], in0=rstd[:, m : m + 1], in1=minus_half[:, m : m + 1], op=ALU.pow
+            )
 
-            for m in range(TOKEN_TILES):
-                nc.scalar.activation(out=gelu[:, m, :], in_=acc[m][:], func=ACT.Gelu)
-            statistics(0)
-            statistics(1)
-            deviation(0)
-            statistics(2)
-            deviation(1)
-            normalise(0)
-            deviation(2)
-            statistics(3)
-            normalise(1)
-            deviation(3)
-            normalise(2)
-            normalise(3)
+        def normalise(m):
+            nc.vector.tensor_scalar(
+                out=gelu[:, m, :],
+                in0=gelu[:, m, :],
+                scalar1=mean_var[:, m, 0:1],
+                scalar2=rstd[:, m : m + 1],
+                op0=ALU.subtract,
+                op1=ALU.mult,
+            )
+            nc.sync.dma_start(out=out_rows[m * P : (m + 1) * P, :], in_=gelu[:, m, :])
+
+        for m in range(TOKEN_TILES):
+            nc.scalar.activation(out=gelu[:, m, :], in_=acc[m][:], func=ACT.Gelu)
+        statistics(0)
+        statistics(1)
+        deviation(0)
+        statistics(2)
+        deviation(1)
+        normalise(0)
+        deviation(2)
+        statistics(3)
+        normalise(1)
+        deviation(3)
+        normalise(2)
+        normalise(3)

@@ -44,6 +44,7 @@ def tile_generatorhead_pa_kernel(tc, hidden, base_w1, spline_w1, out):
         keep = ctx.enter_context(tc.tile_pool(name="keep", bufs=1))
         wload = ctx.enter_context(tc.tile_pool(name="wload", bufs=3))
         fold = ctx.enter_context(tc.tile_pool(name="fold", bufs=3))
+        nears = ctx.enter_context(tc.tile_pool(name="nears", bufs=4))
         once = ctx.enter_context(tc.tile_pool(name="once", bufs=1))
         work = ctx.enter_context(tc.tile_pool(name="work", bufs=2))
         sided = ctx.enter_context(tc.tile_pool(name="sided", bufs=4))
@@ -198,7 +199,7 @@ def tile_generatorhead_pa_kernel(tc, hidden, base_w1, spline_w1, out):
         def folds(u, m, tokens=slice(0, P)):
             i, s = u
             if m == 0 and tokens.start == 0:
-                near[u] = fold.tile([P, WIDTH], F32, name="near")
+                near[u] = nears.tile([P, WIDTH], F32, name="near")
             columns = slice((m * P + tokens.start) * PACK, (m * P + tokens.stop) * PACK)
             nc.scalar.activation(
                 out=near[u][:, columns].rearrange("p (k g) -> p k g", g=PACK),
@@ -474,7 +475,7 @@ def tile_generatorhead_pa_kernel(tc, hidden, base_w1, spline_w1, out):
         inner_product(b)
         drain(2)
         product(before)
-        sides(b)
+        sides_on_scalar(b)
         inner_piece(b)
         join(a)
         drain(2)

@@ -93,8 +93,11 @@ def tile_generatorhead_pa_kernel(tc, hidden, base_w1, spline_w1, out):
 
         ident = keep.tile([P, P], F32)
         make_identity(nc, ident[:])
-        scaled = keep.tile([P, P], BF16)
-        nc.vector.tensor_scalar_mul(out=scaled[:], in0=ident[:], scalar1=1.0 / KNOT_STEP)
+        doubled = keep.tile([P, 2 * P], BF16)
+        for e in range(2):
+            nc.vector.tensor_scalar_mul(
+                out=doubled[:].rearrange("p (k e) -> p k e", e=2)[:, :, e], in0=ident[:], scalar1=1.0 / KNOT_STEP
+            )
         ones = keep.tile([P, P], BF16)
         nc.vector.memset(ones[:], 1.0)
         shift = keep.tile([P, P], BF16)
@@ -109,18 +112,17 @@ def tile_generatorhead_pa_kernel(tc, hidden, base_w1, spline_w1, out):
         zbanks = {}
 
         def make_z(i, m):
-            bank = turns.tile([P, PACK, P], F32, tag="z", name="z")
+            bank = turns.tile([P, 2, P, 2], F32, tag="z", name="z")
             for u in range(2):
                 first = i * CHUNK + u * P
-                for e in range(2):
-                    nc.tensor.matmul(
-                        bank[:, 2 * u + e, :],
-                        lhsT=x_raw[:, m, first : first + P],
-                        rhs=scaled[:],
-                        start=True,
-                        stop=(e == 0),
-                    )
-                nc.tensor.matmul(bank[:, 2 * u + 1, :], lhsT=ones[:], rhs=shift[:], start=False, stop=True)
+                nc.tensor.matmul(
+                    bank[:, u, :, :].rearrange("p k e -> p (k e)"),
+                    lhsT=x_raw[:, m, first : first + P],
+                    rhs=doubled[:],
+                    start=True,
+                    stop=False,
+                )
+                nc.tensor.matmul(bank[:, u, :, 1], lhsT=ones[:], rhs=shift[:], start=False, stop=True)
             zbanks[i, m] = bank
 
         turned = []
@@ -202,8 +204,8 @@ def tile_generatorhead_pa_kernel(tc, hidden, base_w1, spline_w1, out):
                 near[u] = nears.tile([P, WIDTH], F32, name="near")
             columns = slice((m * P + tokens.start) * PACK, (m * P + tokens.stop) * PACK)
             nc.scalar.activation(
-                out=near[u][:, columns].rearrange("p (k g) -> p k g", g=PACK),
-                in_=zbanks[i, m][:, :, tokens].rearrange("p g k -> p k g"),
+                out=near[u][:, columns].rearrange("p (k u e) -> p k u e", u=2, e=2),
+                in_=zbanks[i, m][:, :, tokens, :].rearrange("p u k e -> p k u e"),
                 func=ACT.Abs,
                 bias=1.5 - 2.0 * s,
             )

import math
from contextlib import ExitStack

import concourse.mybir as mybir
from concourse.masks import make_identity

F32 = mybir.dt.float32
BF16 = mybir.dt.bfloat16
U32 = mybir.dt.uint32
U8 = mybir.dt.uint8
FP8X4 = mybir.dt.float8_e4m3fn_x4
ACT = mybir.ActivationFunctionType
ALU = mybir.AluOpType

P = 128
PACK = 4
TOKENS = 512
FEATURES = 1024
OUTS = 512
BASIS = 8
TOKEN_TILES = TOKENS // P
OUT_TILES = OUTS // P
CHUNK = 2 * P
CHUNKS = FEATURES // CHUNK
WIDTH = TOKENS * PACK
WHOLE = slice(0, WIDTH)
QUARTERS = [slice(m * P * PACK, (m + 1) * P * PACK) for m in range(TOKEN_TILES)]
MOST, REST = slice(0, 3 * WIDTH // 4), QUARTERS[3]
EPS = 1e-12
KNOT_STEP = 0.4
KAPPA = math.sqrt(1.0 / 3.0)

FLOPS = 2 * TOKENS * OUTS * (FEATURES + FEATURES * BASIS)


def tile_generatorhead_pa_kernel(tc, hidden, base_w1, spline_w1, out):
    nc = tc.nc
    x_rows = hidden.flatten_outer_dims().rearrange("(m p) i -> p m i", p=P)
    base_rows = base_w1.rearrange("(n p) i -> p n i", p=P)
    spline_rows = spline_w1.rearrange("(n p) i c -> p n (i c)", p=P)
    out_rows = out.flatten_outer_dims()

    with ExitStack() as ctx:
        keep = ctx.enter_context(tc.tile_pool(name="keep", bufs=1))
        wload = ctx.enter_context(tc.tile_pool(name="wload", bufs=3))
        fold = ctx.enter_context(tc.tile_pool(name="fold", bufs=3))
        nears = ctx.enter_context(tc.tile_pool(name="nears", bufs=4))
        once = ctx.enter_context(tc.tile_pool(name="once", bufs=1))
        work = ctx.enter_context(tc.tile_pool(name="work", bufs=2))
        sided = ctx.enter_context(tc.tile_pool(name="sided", bufs=4))
        mx = ctx.enter_context(tc.tile_pool(name="mx", bufs=3))
        wmx = ctx.enter_context(tc.tile_pool(name="wmx", bufs=4))
        acc_pool = ctx.enter_context(tc.psum_pool(name="acc", bufs=1))
        turns = ctx.enter_context(tc.psum_pool(name="turns", bufs=2))

        x_raw = keep.tile([P, TOKEN_TILES, FEATURES], BF16)
        base_raw = keep.tile([P, OUT_TILES, FEATURES], BF16)
        acc = [acc_pool.tile([P, OUTS], F32, name="acc%d" % m) for m in range(TOKEN_TILES)]
        w_raw = {}
        near = {}
        dist = {}
        square = {}
        inner = {}
        neg = {}
        side = {}
        by_scalar = []
        grouped = {}
        quantised = {}

        def partner(u):
            return (u[0], 1 - u[1])

        for tiles, columns in (
            (slice(0, 1), slice(0, CHUNK)),
            (slice(1, TOKEN_TILES), slice(0, CHUNK)),
            (slice(0, TOKEN_TILES), slice(CHUNK, FEATURES)),
        ):
            nc.sync.dma_start(out=x_raw[:, tiles, columns], in_=x_rows[:, tiles, columns])

        def load_weights(i):
            w_raw[i] = wload.tile([P, OUT_TILES, CHUNK * BASIS], BF16, name="w_raw")
            for half in range(2):
                tiles = slice(2 * half, 2 * half + 2)
                nc.sync.dma_start(
                    out=w_raw[i][:, tiles, :],
                    in_=spline_rows[:, tiles, i * CHUNK * BASIS : (i + 1) * CHUNK * BASIS],
                )

        load_weights(0)
        load_weights(1)
        nc.sync.dma_start(out=base_raw[:], in_=base_rows)
        load_weights(2)

        ident = keep.tile([P, P], F32)
        make_identity(nc, ident[:])
        doubled = keep.tile([P, 2 * P], BF16)
        for e in range(2):
            nc.vector.tensor_scalar_mul(
                out=doubled[:].rearrange("p (k e) -> p k e", e=2)[:, :, e], in0=ident[:], scalar1=1.0 / KNOT_STEP
            )
        ones = keep.tile([P, P], BF16)
        nc.vector.memset(ones[:], 1.0)
        shift = keep.tile([P, P], BF16)
        nc.vector.memset(shift[:], -1.0 / P)
        minus_half = keep.tile([P, TOKEN_TILES], F32)
        nc.gpsimd.memset(minus_half[:], -0.5)
        zero = keep.tile([P, 1], F32)
        nc.vector.memset(zero[:], 0.0)
        warm = keep.tile([P, 1], F32)
        nc.scalar.activation(out=warm[:], in_=zero[:], func=ACT.Silu)

        zbanks = {}

        def make_z(i, m):
            bank = turns.tile([P, 2, P, 2], F32, tag="z", name="z")
            for u in range(2):
                first = i * CHUNK + u * P
                nc.tensor.matmul(
                    bank[:, u, :, :].rearrange("p k e -> p (k e)"),
                    lhsT=x_raw[:, m, first : first + P],
                    rhs=doubled[:],
                    start=True,
                    stop=False,
                )
                nc.tensor.matmul(bank[:, u, :, 1], lhsT=ones[:], rhs=shift[:], start=False, stop=True)
            zbanks[i, m] = bank

        turned = []

        def turn(source):
            bank = turns.tile([P, 2, 2, P], F32, tag="w", name="w")
            for n in range(2):
                for u in range(2):
                    nc.tensor.transpose(bank[:, u, n, :], source(n, u), ident[:])
            turned.append(bank)

        def turn_spline(i, s, part, half):
            w = 2 * (1 - part) + s
            words = w_raw[i][:].bitcast(F32).rearrange("p n (f w) -> p n f w", w=BASIS // 2)
            turn(lambda n, u: words[:, 2 * half + n, u * P : (u + 1) * P, w])

        def turn_raw(raw, g, half):
            words = raw[:].bitcast(F32)
            turn(lambda n, u: words[:, 2 * half + n, (2 * g + u) * P : (2 * g + u + 1) * P])

        blocks = []
        for i in range(CHUNKS):
            for s in range(2):
                for part in range(2):
                    for half in range(2):
                        blocks.append((i, s, part, half))

        others = [(raw, g, half) for raw in (base_raw, x_raw) for g in range(2) for half in range(2)]

        def fill(count=1):
            for j in range(count):
                if blocks:
                    turn_spline(*blocks.pop(0))
                elif others:
                    turn_raw(*others.pop(0))

        drained = []

        def drain(count=1):
            for j in range(count):
                step = len(drained)
                key = ("w", step // 8, (step // 4) % 2)
                part, half = (step // 2) % 2, step % 2
                if part == 0 and half == 0:
                    grouped[key] = work.tile([P, 2, OUTS, PACK], BF16, align_bytes=64, tag="w_grouped", name="w_grouped")
                copy_words(grouped[key][:, part, :, :], half, turned.pop(0))
                drained.append(step)
                fill()

        def copy_words(target, half, bank):
            rows = target[:, half * 2 * P : (half + 1) * 2 * P, :].bitcast(F32)
            nc.scalar.copy(out=rows, in_=bank[:].rearrange("p u n k -> p (n k) u"))

        def drain_base():
            grouped["base"] = work.tile([P, 2, OUTS, PACK], BF16, align_bytes=64, tag="w_grouped", name="base_grouped")
            for g in range(2):
                for half in range(2):
                    copy_words(grouped["base"][:, g, :, :], half, turned.pop(0))
                    fill()

        def drain_silu():
            grouped["silu"] = work.tile([P, 2, TOKENS, PACK], BF16, align_bytes=64, tag="w_grouped", name="silu")
            for g in range(2):
                for half in range(2):
                    bank = turned.pop(0)
                    pairs = bank[:].rearrange("p u n k -> p u (n k)").bitcast(BF16)
                    nc.scalar.activation(
                        out=grouped["silu"][:, g, half * 2 * P : (half + 1) * 2 * P, :].rearrange(
                            "p k (u e) -> p k u e", u=2
                        ),
                        in_=pairs.rearrange("p u (k e) -> p k u e", e=2),
                        func=ACT.Silu,
                    )
                    fill()

        def folds(u, m, tokens=slice(0, P)):
            i, s = u
            if m == 0 and tokens.start == 0:
                near[u] = nears.tile([P, WIDTH], F32, name="near")
            columns = slice((m * P + tokens.start) * PACK, (m * P + tokens.stop) * PACK)
            nc.scalar.activation(
                out=near[u][:, columns].rearrange("p (k u e) -> p k u e", u=2, e=2),
                in_=zbanks[i, m][:, :, tokens, :].rearrange("p u k e -> p k u e"),
                func=ACT.Abs,
                bias=1.5 - 2.0 * s,
            )

        def refold(u, part=WHOLE):
            if part.start == 0:
                dist[u] = fold.tile([P, WIDTH], F32, name="dist")
            nc.scalar.activation(out=dist[u][:, part], in_=near[u][:, part], func=ACT.Abs, bias=-2.0)

        def squares(u, part=WHOLE):
            if part.start == 0:
                square[u] = fold.tile([P, WIDTH], F32, name="square")
            nc.scalar.activation(
                out=square[u][:, part], in_=dist[u][:, part], func=ACT.Square, scale=-KAPPA, bias=2.0 * KAPPA
            )

        def outer_piece(u, part=WHOLE):
            if part.start == 0:
                neg[u] = work.tile([P, WIDTH], BF16, name="neg")
            nc.vector.scalar_tensor_tensor(
                out=neg[u][:, part],
                in0=dist[u][:, part],
                scalar=2.0,
                in1=square[u][:, part],
                op0=ALU.subtract,
                op1=ALU.mult,
            )

        def inner_product(u, part=WHOLE):
            other = square[partner(u)]
            nc.vector.scalar_tensor_tensor(
                out=other[:, part],
                in0=dist[u][:, part],
                scalar=2.0,
                in1=other[:, part],
                op0=ALU.subtract,
                op1=ALU.mult,
            )

        def inner_piece(u, on_scalar=True, part=WHOLE):
            if part.start == 0:
                inner[u] = work.tile([P, WIDTH], BF16, name="inner")
            source = square[partner(u)][:, part]
            if on_scalar:
                nc.scalar.activation(
                    out=inner[u][:, part], in_=source, func=ACT.Identity, scale=-3.0, bias=-4.0 / 3.0
                )
            else:
                nc.vector.tensor_scalar(
                    out=inner[u][:, part], in0=source, scalar1=-3.0, scalar2=-4.0 / 3.0, op0=ALU.mult, op1=ALU.add
                )

        def sides(u, part=WHOLE):
            if part.start == 0:
                side[u] = sided.tile([P, WIDTH], BF16, name="side")
            nc.vector.tensor_scalar(
                out=side[u][:, part],
                in0=near[partner(u)][:, part],
                scalar1=2.0,
                scalar2=0.5,
                op0=ALU.is_le if u[1] == 0 else ALU.is_ge,
                op1=ALU.subtract,
            )

        def sides_on_scalar(u):
            side[u] = sided.tile([P, WIDTH], BF16, name="side")
            by_scalar.append(u)
            turned_round = u[1] == 0
            nc.scalar.activation(
                out=side[u][:],
                in_=near[partner(u)][:],
                func=ACT.Sign,
                scale=-1.0 if turned_round else 1.0,
                bias=2.0 if turned_round else -2.0,
            )

        def size(u):
            return 0.5 if u in by_scalar else 1.0

        def join(u, part=WHOLE):
            values = neg[u][:, part]
            nc.vector.tensor_tensor(out=values, in0=values, in1=inner[u][:, part], op=ALU.max)

        def clip(u, part=WHOLE):
            values = neg[u][:, part]
            nc.vector.tensor_scalar_min(out=values, in0=values, scalar1=0.0)

        def sign(u, part=WHOLE):
            values = neg[u][:, part]
            nc.vector.tensor_tensor(out=values, in0=values, in1=side[u][:, part], op=ALU.mult)

        def split(u, part=WHOLE):
            if part.start == 0:
                grouped[u] = once.tile([P, 2, WIDTH], BF16, align_bytes=64, name="basis")
            nc.vector.tensor_scalar(
                out=grouped[u][:, 0, part], in0=neg[u][:, part], scalar1=-size(u), scalar2=0.0, op0=ALU.mult, op1=ALU.max
            )
            nc.vector.tensor_scalar(
                out=grouped[u][:, 1, part], in0=neg[u][:, part], scalar1=size(u), scalar2=0.0, op0=ALU.mult, op1=ALU.max
            )

        def quantise(pool, key, source, columns):
            if columns.start == 0 and key not in quantised:
                codes = pool.tile([P, 2 * OUTS], U32, align_bytes=64, name="codes")
                scales = pool.tile([P, 2 * OUTS], U8, align_bytes=64, name="scales")
                quantised[key] = (codes, scales)
            codes, scales = quantised[key]
            words = slice(columns.start // PACK, columns.stop // PACK)
            nc.vector.quantize_mx(
                out=codes[:, words].bitcast(FP8X4), scales=scales[:, words], in_=source[:, columns]
            )

        def quantise_unit(u):
            quantise(mx, u, grouped[u][:].rearrange("p h k -> p (h k)"), slice(0, 2 * WIDTH))

        def quantise_pieces(u, pieces):
            for piece in pieces:
                for h in range(2):
                    quantise(
                        mx,
                        u,
                        grouped[u][:].rearrange("p h k -> p (h k)"),
                        slice(h * WIDTH + piece.start, h * WIDTH + piece.stop),
                    )

        def quantise_weights(key):
            quantise(wmx, key, grouped[key][:].rearrange("p h o t -> p (h o t)"), slice(0, 2 * WIDTH))

        opened = []

        def contract(act_key, w_key, tiles=range(TOKEN_TILES), last=False):
            act_codes, act_scales = quantised[act_key]
            w_codes, w_scales = quantised[w_key]
            for m in tiles:
                for h in range(2):
                    cols = slice(h * TOKENS + m * P, h * TOKENS + (m + 1) * P)
                    outs = slice(h * OUTS, (h + 1) * OUTS)
                    nc.tensor.matmul_mx(
                        out=acc[m][:],
                        lhsT=act_codes[:, cols].bitcast(FP8X4),
                        lhsT_scale=act_scales[:, cols],
                        rhs=w_codes[:, outs].bitcast(FP8X4),
                        rhs_scale=w_scales[:, outs],
                        start=m not in opened,
                        stop=last and h == 1,
                    )
                    opened.append(m)

        def product(u, tiles=range(TOKEN_TILES), last=False):
            contract(u, ("w", u[0], u[1]), tiles, last)

        with tc.manual_schedule():
            a, b = (0, 0), (0, 1)
            make_z(0, 0)
            make_z(0, 1)
            fill(2)
            halves = (slice(0, P // 2), slice(P // 2, P))
            steps = [(0, halves[0]), (0, halves[1])] + [(m, slice(0, P)) for m in range(1, TOKEN_TILES)]
            for step in range(len(steps)):
                m, tokens = steps[step]
                part = slice((m * P + tokens.start) * PACK, (m * P + tokens.stop) * PACK)
                folds(b, m, tokens)
                folds(a, m, tokens)
                if tokens.stop == P and m + 2 < TOKEN_TILES:
                    make_z(0, m + 2)
                refold(b, part)
                refold(a, part)
                squares(b, part)
                squares(a, part)
                if m > 0:
                    sides(a, QUARTERS[m - 1])
                    inner_piece(a, False, QUARTERS[m - 1])
                    sides(b, QUARTERS[m - 1])
                    inner_piece(b, False, QUARTERS[m - 1])
                if m == 3:
                    sides(a, QUARTERS[3])
                    sides(b, QUARTERS[3])
                outer_piece(b, part)
                inner_product(a, part)
                outer_piece(a, part)
                inner_product(b, part)
            make_z(1, 0)
            make_z(1, 1)
            inner_piece(a, False, QUARTERS[3])
            inner_piece(b, False, QUARTERS[3])

        before = None
        for i in range(CHUNKS - 1):
            a, b = (i, 0), (i, 1)
            a1, b1 = (i + 1, 0), (i + 1, 1)
            if before:
                outer_piece(b)
                quantise_unit(before)
            folds(b1, 0)
            folds(a1, 0)
            make_z(i + 1, 2)
            if before:
                inner_product(a)
            drain(2)
            folds(b1, 1)
            folds(a1, 1)
            make_z(i + 1, 3)
            folds(b1, 2)
            folds(a1, 2)
            if before:
                inner_piece(a)
                outer_piece(a)
                inner_product(b)
            drain(2)
            if before:
                product(before)
            folds(b1, 3)
            folds(a1, 3)
            if before:
                inner_piece(b)
            join(a)
            if i == 0:
                join(b)
            else:
                quantise_weights(("w", i, 0))
            clip(a)
            if i > 0:
                join(b)
            refold(b1)
            drain(2)
            if i == 0:
                clip(b)
            sign(a)
            if i == 0:
                sign(b)
            else:
                clip(b)
            split(a)
            if i < 2:
                sides(b1)
            if i == 0:
                quantise_weights(("w", i, 0))
            quantise_unit(a)
            refold(a1)
            if i > 0:
                sign(b)
            if i == 0:
                sides(a1)
            if i == 1:
                sides_on_scalar(a1)
            drain(2)
            if i + 2 < CHUNKS:
                make_z(i + 2, 0)
                make_z(i + 2, 1)
            product(a)
            squares(b1)
            squares(a1)
            split(b)
            quantise_weights(("w", i, 1))
            if i + 3 < CHUNKS:
                load_weights(i + 3)
            before = b

        a, b = (CHUNKS - 1, 0), (CHUNKS - 1, 1)
        drain(2)
        outer_piece(b)
        sides_on_scalar(a)
        quantise_unit(before)
        inner_product(a)
        drain(2)
        inner_piece(a)
        outer_piece(a)
        quantise_weights(("w", CHUNKS - 1, 0))
        inner_product(b)
        drain(2)
        product(before)
        sides_on_scalar(b)
        inner_piece(b)
        join(a)
        drain(2)
        drain_base()
        clip(a)
        join(b, MOST)
        sign(a)
        clip(b, MOST)
        drain_silu()
        split(a)
        quantise_weights(("w", CHUNKS - 1, 1))
        quantise_unit(a)
        quantise_weights("base")
        product(a)
        sign(b, MOST)
        quantise(mx, "silu", grouped["silu"][:].rearrange("p g k t -> p (g k t)"), slice(0, 2 * WIDTH))
        contract("silu", "base")
        split(b, MOST)
        join(b, REST)
        quantise_pieces(b, (slice(0, WIDTH // 2), QUARTERS[2]))
        product(b, (0, 1, 2), last=True)
        clip(b, REST)
        sign(b, REST)
        split(b, REST)
        quantise_pieces(b, (QUARTERS[3],))
        product(b, (3,), last=True)

        nc.scalar.activation(out=warm[:], in_=grouped["silu"][:, 1, TOKENS - 1, 0:1], func=ACT.Gelu)
        stats = keep.tile([P, TOKEN_TILES, 6], F32)
        mean_var = keep.tile([P, TOKEN_TILES, 2], F32)
        rstd = keep.tile([P, TOKEN_TILES], F32)
        gelu = fold.tile([P, TOKEN_TILES, OUTS], F32, tag="dist", name="gelu")

        def statistics(m):
            nc.vector.bn_stats(out=stats[:, m, :], in_=gelu[:, m, :])

        def deviation(m):
            nc.vector.bn_aggr(out=mean_var[:, m, :], in_=stats[:, m, :])
            nc.gpsimd.tensor_scalar(
                out=rstd[:, m : m + 1],
                in0=mean_var[:, m, 1:2],
                scalar1=EPS,
                scalar2=0.0,
                op0=ALU.add,
                op1=ALU.add,
            )
            nc.gpsimd.tensor_tensor(
                out=rstd[:, m : m + 1], in0=rstd[:, m : m + 1], in1=minus_half[:, m : m + 1], op=ALU.pow
            )

        def normalise(m):
            nc.vector.tensor_scalar(
                out=gelu[:, m, :],
                in0=gelu[:, m, :],
                scalar1=mean_var[:, m, 0:1],
                scalar2=rstd[:, m : m + 1],
                op0=ALU.subtract,
                op1=ALU.mult,
            )
            nc.sync.dma_start(out=out_rows[m * P : (m + 1) * P, :], in_=gelu[:, m, :])

        for m in range(TOKEN_TILES):
            nc.scalar.activation(out=gelu[:, m, :], in_=acc[m][:], func=ACT.Gelu)
        statistics(0)
        statistics(1)
        deviation(0)
        statistics(2)
        deviation(1)
        normalise(0)
        deviation(2)
        statistics(3)
        normalise(1)
        deviation(3)
        normalise(2)
        normalise(3)
